import numpy as np
import ml_dtypes


def mxq(x, axis, fmt="e4m3"):
    dtype, down = {"e4m3": (ml_dtypes.float8_e4m3fn, 7), "e5m2": (ml_dtypes.float8_e5m2, 14)}[fmt]
    v = np.moveaxis(np.asarray(x, np.float32).astype(ml_dtypes.bfloat16).astype(np.float64), axis, -1)
    blocks = v.reshape(v.shape[:-1] + (-1, 32))
    amax = np.abs(blocks).max(-1, keepdims=True)
    byte = np.maximum(np.where(amax > 0, np.frexp(amax)[1] - 1 + 127, 0) - down, 1)
    scale = np.exp2(byte - 127.0)
    codes = (blocks / scale).astype(np.float32).astype(dtype).astype(np.float64)
    return np.moveaxis((codes * scale).reshape(v.shape), -1, axis)


WIDE = False


def mx_kscale(k):
    if not WIDE:
        return np.ones(k)
    levels = np.array([10, -10, 5, -5, 0])
    a = np.random.permutation(np.resize(levels, k // 512 * 4)).reshape(k // 512, 4)
    idx = np.arange(k)
    return np.exp2(a[idx // 512, idx % 128 // 32])


BF16 = ml_dtypes.bfloat16


def bf(x):
    return np.asarray(x, np.float32).astype(BF16)


def f64(x):
    return np.asarray(x).astype(np.float64)


E, B, STATE, ACTION, H0, H1, H2, H3 = 7, 1024, 128, 8, 256, 256, 1024, 512


def swish(v):
    return v * (1.0 / (1.0 + np.exp(-v)))


def softplus(v):
    return np.maximum(v, 0.0) + np.log(1.0 + np.exp(-np.abs(v)))


def soft_clamp(x, lo, hi):
    x = hi - softplus(hi - x)
    x = lo + softplus(x - lo)
    return x


def setup_inputs():
    s = mx_kscale(H2)
    return {
        "h2": bf(swish(np.random.standard_normal((E, B, H2))) * s),
        "W3": bf(np.random.standard_normal((E, H2, H3)) * 1.5 / np.sqrt(H2) / s[None, :, None]),
        "b3": bf(np.random.standard_normal((E, H3)) * 0.2),
        "Wmu": bf(np.random.standard_normal((E, H3, STATE)) * 1.5 / np.sqrt(H3)),
        "bmu": bf(np.random.standard_normal((E, STATE)) * 0.2),
        "Wsig": bf(np.random.standard_normal((E, H3, STATE)) * 2.5 / np.sqrt(H3)),
        "bsig": bf(np.random.standard_normal((E, STATE)) * 0.2),
        "max_logstd": bf(1.0 + 0.2 * np.random.standard_normal(STATE)),
        "min_logstd": bf(-1.0 + 0.2 * np.random.standard_normal(STATE)),
        "state": bf(np.random.standard_normal((B, STATE))),
    }


def reference(h2, W3, b3, Wmu, bmu, Wsig, bsig, max_logstd, min_logstd, state):
    h = swish((mxq(f64(h2), 2, "e4m3") @ mxq(f64(W3), 1, "e4m3")) + f64(b3)[:, None, :])
    hq = mxq(h, 2, "e4m3")
    mu = (hq @ mxq(f64(Wmu), 1, "e4m3")) + f64(bmu)[:, None, :]
    log_sigma = (hq @ mxq(f64(Wsig), 1, "e4m3")) + f64(bsig)[:, None, :]
    log_sigma = soft_clamp(log_sigma, f64(min_logstd), f64(max_logstd))
    sigma = np.exp(log_sigma)
    mu = mu + f64(state)[None, :, :]
    return mu, sigma

@@ -1,0 +1,254 @@
+from contextlib import ExitStack
+
+import concourse.mybir as mybir
+from concourse.masks import make_identity
+
+F32 = mybir.dt.float32
+BF16 = mybir.dt.bfloat16
+U32 = mybir.dt.uint32
+U8 = mybir.dt.uint8
+FP8X4 = mybir.dt.float8_e4m3fn_x4
+ACT = mybir.ActivationFunctionType
+ALU = mybir.AluOpType
+
+MEMBERS = 7
+BATCH = 1024
+K1 = 1024
+K2 = 512
+STATE = 128
+
+P = 128
+PACK = 4
+K_PASS = P * PACK
+PASSES1 = K1 // K_PASS
+H_TILES = K2 // P
+ROWS_PER_PARTITION = BATCH // P
+UNIT = 512
+BLOCKS = UNIT // P
+UNITS = BATCH // UNIT
+WORDS = K1 // 2
+HEADS = 2
+RUN = 4
+
+ROW_B3 = 0
+ROW_BMU = ROW_B3 + MEMBERS * H_TILES
+ROW_BSIG = ROW_BMU + MEMBERS
+ROW_MAX = ROW_BSIG + MEMBERS
+ROW_MIN = ROW_MAX + 1
+
+FLOPS = 2 * MEMBERS * BATCH * (K1 * K2 + K2 * HEADS * STATE)
+
+
+def tile_ensembledynamicmodel_pa_t_kernel(
+    tc, h2, W3, b3, Wmu, bmu, Wsig, bsig, max_logstd, min_logstd, state, out_0, out_1
+):
+    nc = tc.nc
+
+    def regroup(dst, src):
+        nc.vector.tensor_copy(
+            out=dst.rearrange("p (c i) t -> p c t i", i=RUN),
+            in_=src.rearrange("p t (c i) -> p c t i", i=RUN),
+        )
+
+    def quantise(codes, scales, grouped):
+        nc.vector.quantize_mx(out=codes.bitcast(FP8X4), scales=scales, in_=grouped)
+
+    with ExitStack() as ctx:
+        consts = ctx.enter_context(tc.tile_pool(name="consts", bufs=1))
+        h2_pool = ctx.enter_context(tc.tile_pool(name="h2_pool", bufs=4))
+        weights = ctx.enter_context(tc.tile_pool(name="weights", bufs=2))
+        work = ctx.enter_context(tc.tile_pool(name="work", bufs=3))
+        results = ctx.enter_context(tc.tile_pool(name="results", bufs=3))
+        psum = ctx.enter_context(tc.psum_pool(name="psum", bufs=2))
+
+        ident_f32 = consts.tile([P, P], F32)
+        make_identity(nc, ident_f32[:])
+        ident_bf16 = consts.tile([P, P], BF16)
+        make_identity(nc, ident_bf16[:])
+
+        rows = consts.tile([P, P], BF16)
+        nc.vector.memset(rows[:], 0.0)
+        nc.scalar.dma_start(
+            out=rows[ROW_B3:ROW_BMU, :], in_=b3.rearrange("e (t p) -> (e t) p", p=P)
+        )
+        nc.scalar.dma_start(out=rows[ROW_BMU:ROW_BSIG, :], in_=bmu)
+        nc.scalar.dma_start(out=rows[ROW_BSIG:ROW_MAX, :], in_=bsig)
+        nc.scalar.dma_start(
+            out=rows[ROW_MAX : ROW_MAX + 1, :], in_=max_logstd.rearrange("(o s) -> o s", o=1)
+        )
+        nc.scalar.dma_start(
+            out=rows[ROW_MIN : ROW_MIN + 1, :], in_=min_logstd.rearrange("(o s) -> o s", o=1)
+        )
+        state_sb = consts.tile([P, ROWS_PER_PARTITION, STATE], BF16)
+        nc.scalar.dma_start(
+            out=state_sb[:], in_=state.rearrange("(p j) s -> p j s", j=ROWS_PER_PARTITION)
+        )
+
+        cols_ps = psum.tile([P, P], BF16, tag="back")
+        nc.tensor.transpose(cols_ps[:], rows[:], ident_bf16[:])
+        cols = consts.tile([P, P], F32)
+        nc.vector.tensor_copy(out=cols[:], in_=cols_ps[:])
+
+        tanh_bias = consts.tile([P, MEMBERS], F32)
+        nc.vector.tensor_scalar(
+            out=tanh_bias[:],
+            in0=cols[:, ROW_BSIG:ROW_MAX],
+            scalar1=cols[:, ROW_MAX : ROW_MAX + 1],
+            scalar2=0.5,
+            op0=ALU.subtract,
+            op1=ALU.mult,
+        )
+        exp_bounds = consts.tile([P, 2], F32)
+        nc.scalar.activation(out=exp_bounds[:], in_=cols[:, ROW_MAX : ROW_MIN + 1], func=ACT.Exp)
+        sigma_scale = consts.tile([P, 1], F32)
+        nc.vector.tensor_scalar(
+            out=sigma_scale[:], in0=exp_bounds[:, 0:1], scalar1=0.5, scalar2=None, op0=ALU.mult
+        )
+        sigma_shift = consts.tile([P, 1], F32)
+        nc.vector.tensor_tensor(
+            out=sigma_shift[:], in0=sigma_scale[:], in1=exp_bounds[:, 1:2], op=ALU.add
+        )
+
+        for e in range(MEMBERS):
+            w3_raw = weights.tile([P, 2 * PASSES1, 2 * K2], BF16)
+            nc.sync.dma_start(
+                out=w3_raw[:], in_=W3[e].rearrange("(a q r) c -> q a (r c)", q=P, r=2)
+            )
+            w3_rows = w3_raw[:].rearrange("p a (r c) -> p (a r) c", r=2)
+            w3_grouped = weights.tile([P, PASSES1, K2, PACK], BF16, align_bytes=64)
+            for g in range(PASSES1):
+                regroup(w3_grouped[:, g], w3_rows[:, PACK * g : PACK * (g + 1), :])
+            w3_codes = weights.tile([P, PASSES1 * K2], U32, align_bytes=64)
+            w3_scales = weights.tile([P, PASSES1 * K2], U8, align_bytes=64)
+            quantise(w3_codes[:], w3_scales[:], w3_grouped[:].rearrange("p g c t -> p (g c t)"))
+
+            w2_raw = weights.tile([P, HEADS, PACK, STATE], BF16)
+            nc.sync.dma_start(out=w2_raw[:, 0], in_=Wmu[e].rearrange("(t p) s -> p t s", p=P))
+            nc.sync.dma_start(out=w2_raw[:, 1], in_=Wsig[e].rearrange("(t p) s -> p t s", p=P))
+            w2_grouped = weights.tile([P, HEADS, STATE, PACK], BF16, align_bytes=64)
+            for head in range(HEADS):
+                regroup(w2_grouped[:, head], w2_raw[:, head])
+            w2_codes = weights.tile([P, HEADS * STATE], U32, align_bytes=64)
+            w2_scales = weights.tile([P, HEADS * STATE], U8, align_bytes=64)
+            quantise(w2_codes[:], w2_scales[:], w2_grouped[:].rearrange("p w s t -> p (w s t)"))
+
+            for n in range(UNITS):
+                unit_rows = slice(BLOCKS * n, BLOCKS * (n + 1))
+
+                h2_raw = h2_pool.tile([P, BLOCKS * K1], BF16)
+                nc.sync.dma_start(
+                    out=h2_raw[:].rearrange("p (j k) -> p j k", j=BLOCKS),
+                    in_=h2[e].rearrange("(p j) k -> p j k", j=ROWS_PER_PARTITION)[:, unit_rows, :],
+                )
+                h2_words = h2_raw[:].bitcast(F32)
+                h2_grouped = work.tile([P, PASSES1 * UNIT * PACK], BF16, align_bytes=64)
+                h2_grouped_words = (
+                    h2_grouped[:].bitcast(F32).rearrange("p (g b u) -> p g b u", g=PASSES1, u=2)
+                )
+                for j in range(BLOCKS):
+                    flipped = psum.tile([P, 2 * PASSES1, P], F32, tag="flipped")
+                    for a in range(2 * PASSES1):
+                        first = j * WORDS + a * P
+                        nc.tensor.transpose(
+                            flipped[:, a, :], h2_words[:, first : first + P], ident_f32[:]
+                        )
+                    nc.scalar.copy(
+                        out=h2_grouped_words[:, :, j * P : (j + 1) * P, :],
+                        in_=flipped[:].rearrange("p (g u) b -> p g b u", u=2),
+                    )
+                h2_codes = work.tile([P, PASSES1 * UNIT], U32, align_bytes=64)
+                h2_scales = work.tile([P, PASSES1 * UNIT], U8, align_bytes=64)
+                quantise(h2_codes[:], h2_scales[:], h2_grouped[:])
+
+                h_tiles = work.tile([P, H_TILES, UNIT], BF16)
+                for m in range(H_TILES):
+                    acc1 = psum.tile([P, UNIT], F32, tag="acc1")
+                    for g in range(PASSES1):
+                        w_cols = slice(g * K2 + m * P, g * K2 + (m + 1) * P)
+                        x_cols = slice(g * UNIT, (g + 1) * UNIT)
+                        nc.tensor.matmul_mx(
+                            out=acc1[:],
+                            lhsT=w3_codes[:, w_cols].bitcast(FP8X4),
+                            lhsT_scale=w3_scales[:, w_cols],
+                            rhs=h2_codes[:, x_cols].bitcast(FP8X4),
+                            rhs_scale=h2_scales[:, x_cols],
+                            start=(g == 0),
+                            stop=(g == PASSES1 - 1),
+                        )
+                    b3_col = ROW_B3 + e * H_TILES + m
+                    nc.scalar.activation(
+                        out=h_tiles[:, m, :],
+                        in_=acc1[:],
+                        func=ACT.Silu,
+                        bias=cols[:, b3_col : b3_col + 1],
+                        scale=1.0,
+                    )
+                h_grouped = work.tile([P, UNIT, PACK], BF16, align_bytes=64)
+                regroup(h_grouped[:], h_tiles[:])
+                h_codes = work.tile([P, UNIT], U32, align_bytes=64)
+                h_scales = work.tile([P, UNIT], U8, align_bytes=64)
+                quantise(h_codes[:], h_scales[:], h_grouped[:].rearrange("p b t -> p (b t)"))
+
+                heads_t = []
+                for head in range(HEADS):
+                    acc2 = psum.tile([P, UNIT], F32, tag="acc2")
+                    w_cols = slice(head * STATE, (head + 1) * STATE)
+                    nc.tensor.matmul_mx(
+                        out=acc2[:],
+                        lhsT=w2_codes[:, w_cols].bitcast(FP8X4),
+                        lhsT_scale=w2_scales[:, w_cols],
+                        rhs=h_codes[:].bitcast(FP8X4),
+                        rhs_scale=h_scales[:],
+                        start=True,
+                        stop=True,
+                    )
+                    heads_t.append(acc2)
+
+                mu_t = work.tile([P, UNIT], F32)
+                nc.scalar.activation(
+                    out=mu_t[:],
+                    in_=heads_t[0][:],
+                    func=ACT.Identity,
+                    bias=cols[:, ROW_BMU + e : ROW_BMU + e + 1],
+                    scale=1.0,
+                )
+                sigma_t = work.tile([P, UNIT], F32)
+                nc.scalar.activation(
+                    out=sigma_t[:],
+                    in_=heads_t[1][:],
+                    func=ACT.Tanh,
+                    bias=tanh_bias[:, e : e + 1],
+                    scale=0.5,
+                )
+                nc.vector.tensor_scalar(
+                    out=sigma_t[:],
+                    in0=sigma_t[:],
+                    scalar1=sigma_scale[:, 0:1],
+                    scalar2=sigma_shift[:, 0:1],
+                    op0=ALU.mult,
+                    op1=ALU.add,
+                )
+
+                mu_back = psum.tile([P, BLOCKS, STATE], F32, tag="back")
+                for j in range(BLOCKS):
+                    nc.tensor.transpose(mu_back[:, j, :], mu_t[:, j * P : (j + 1) * P], ident_f32[:])
+                mu_out = results.tile([P, BLOCKS, STATE], F32)
+                nc.vector.tensor_tensor(
+                    out=mu_out[:], in0=mu_back[:], in1=state_sb[:, unit_rows, :], op=ALU.add
+                )
+                nc.sync.dma_start(
+                    out=out_0[e].rearrange("(p j) s -> p j s", j=ROWS_PER_PARTITION)[:, unit_rows, :],
+                    in_=mu_out[:],
+                )
+
+                sigma_back = psum.tile([P, BLOCKS, STATE], F32, tag="back")
+                for j in range(BLOCKS):
+                    nc.tensor.transpose(
+                        sigma_back[:, j, :], sigma_t[:, j * P : (j + 1) * P], ident_f32[:]
+                    )
+                sigma_out = results.tile([P, BLOCKS, STATE], F32)
+                nc.scalar.copy(out=sigma_out[:], in_=sigma_back[:])
+                nc.sync.dma_start(
+                    out=out_1[e].rearrange("(p j) s -> p j s", j=ROWS_PER_PARTITION)[:, unit_rows, :],
+                    in_=sigma_out[:],
+                )

@@ -26,8 +26,10 @@ ROWS_PER_PARTITION = BATCH // P
 UNIT = 512
 BLOCKS = UNIT // P
 UNITS = BATCH // UNIT
+N_UNITS = MEMBERS * UNITS
 WORDS = K1 // 2
 HEADS = 2
+RING = 4
 RUN = 4
 
 ROW_B3 = 0
@@ -60,6 +62,7 @@ def tile_ensembledynamicmodel_pa_t_kernel(
         work = ctx.enter_context(tc.tile_pool(name="work", bufs=3))
         results = ctx.enter_context(tc.tile_pool(name="results", bufs=3))
         psum = ctx.enter_context(tc.psum_pool(name="psum", bufs=2))
+        ctx.enter_context(tc.manual_schedule())
 
         ident_f32 = consts.tile([P, P], F32)
         make_identity(nc, ident_f32[:])
@@ -101,154 +104,231 @@ def tile_ensembledynamicmodel_pa_t_kernel(
         exp_bounds = consts.tile([P, 2], F32)
         nc.scalar.activation(out=exp_bounds[:], in_=cols[:, ROW_MAX : ROW_MIN + 1], func=ACT.Exp)
         sigma_scale = consts.tile([P, 1], F32)
-        nc.vector.tensor_scalar(
-            out=sigma_scale[:], in0=exp_bounds[:, 0:1], scalar1=0.5, scalar2=None, op0=ALU.mult
-        )
+        nc.scalar.mul(out=sigma_scale[:], in_=exp_bounds[:, 0:1], mul=0.5)
         sigma_shift = consts.tile([P, 1], F32)
-        nc.vector.tensor_tensor(
-            out=sigma_shift[:], in0=sigma_scale[:], in1=exp_bounds[:, 1:2], op=ALU.add
+        nc.scalar.activation(
+            out=sigma_shift[:],
+            in_=exp_bounds[:, 1:2],
+            func=ACT.Identity,
+            bias=sigma_scale[:, 0:1],
+            scale=1.0,
         )
+        table_warmer = consts.tile([P, 1], F32)
+        nc.scalar.activation(out=table_warmer[:], in_=sigma_shift[:], func=ACT.Silu)
 
-        for e in range(MEMBERS):
+        raw_weights, grouped_w3, stage1_weights, stage2_weights = {}, {}, {}, {}
+        h2_loaded, h2_flipped, h2_quantised = {}, {}, {}
+        h_plain, h_regrouped, h_quantised = {}, {}, {}
+        mu_transposed, sigma_transposed, mu_banks, sigma_banks = {}, {}, {}, {}
+
+        def batch_rows(dram, u):
+            e, n = divmod(u, UNITS)
+            by_partition = dram[e].rearrange("(p j) x -> p j x", j=ROWS_PER_PARTITION)
+            return by_partition[:, BLOCKS * n : BLOCKS * (n + 1), :]
+
+        def load_weights(e):
             w3_raw = weights.tile([P, 2 * PASSES1, 2 * K2], BF16)
             nc.sync.dma_start(
                 out=w3_raw[:], in_=W3[e].rearrange("(a q r) c -> q a (r c)", q=P, r=2)
             )
+            w2_raw = weights.tile([P, HEADS, PACK, STATE], BF16)
+            nc.sync.dma_start(out=w2_raw[:, 0], in_=Wmu[e].rearrange("(t p) s -> p t s", p=P))
+            nc.sync.dma_start(out=w2_raw[:, 1], in_=Wsig[e].rearrange("(t p) s -> p t s", p=P))
+            raw_weights[e] = (w3_raw, w2_raw)
+
+        def regroup_w3(e):
+            w3_raw = raw_weights[e][0]
             w3_rows = w3_raw[:].rearrange("p a (r c) -> p (a r) c", r=2)
             w3_grouped = weights.tile([P, PASSES1, K2, PACK], BF16, align_bytes=64)
             for g in range(PASSES1):
                 regroup(w3_grouped[:, g], w3_rows[:, PACK * g : PACK * (g + 1), :])
-            w3_codes = weights.tile([P, PASSES1 * K2], U32, align_bytes=64)
-            w3_scales = weights.tile([P, PASSES1 * K2], U8, align_bytes=64)
-            quantise(w3_codes[:], w3_scales[:], w3_grouped[:].rearrange("p g c t -> p (g c t)"))
+            grouped_w3[e] = w3_grouped
 
-            w2_raw = weights.tile([P, HEADS, PACK, STATE], BF16)
-            nc.sync.dma_start(out=w2_raw[:, 0], in_=Wmu[e].rearrange("(t p) s -> p t s", p=P))
-            nc.sync.dma_start(out=w2_raw[:, 1], in_=Wsig[e].rearrange("(t p) s -> p t s", p=P))
+        def quantise_weights(e):
+            w2_raw = raw_weights[e][1]
             w2_grouped = weights.tile([P, HEADS, STATE, PACK], BF16, align_bytes=64)
             for head in range(HEADS):
                 regroup(w2_grouped[:, head], w2_raw[:, head])
+            w3_codes = weights.tile([P, PASSES1 * K2], U32, align_bytes=64)
+            w3_scales = weights.tile([P, PASSES1 * K2], U8, align_bytes=64)
+            quantise(w3_codes[:], w3_scales[:], grouped_w3[e][:].rearrange("p g c t -> p (g c t)"))
+            stage1_weights[e] = (w3_codes, w3_scales)
             w2_codes = weights.tile([P, HEADS * STATE], U32, align_bytes=64)
             w2_scales = weights.tile([P, HEADS * STATE], U8, align_bytes=64)
             quantise(w2_codes[:], w2_scales[:], w2_grouped[:].rearrange("p w s t -> p (w s t)"))
+            stage2_weights[e] = (w2_codes, w2_scales)
 
-            for n in range(UNITS):
-                unit_rows = slice(BLOCKS * n, BLOCKS * (n + 1))
+        def load_h2(u):
+            h2_raw = h2_pool.tile([P, BLOCKS * K1], BF16)
+            nc.sync.dma_start(
+                out=h2_raw[:].rearrange("p (j k) -> p j k", j=BLOCKS), in_=batch_rows(h2, u)
+            )
+            h2_loaded[u] = h2_raw
 
-                h2_raw = h2_pool.tile([P, BLOCKS * K1], BF16)
-                nc.sync.dma_start(
-                    out=h2_raw[:].rearrange("p (j k) -> p j k", j=BLOCKS),
-                    in_=h2[e].rearrange("(p j) k -> p j k", j=ROWS_PER_PARTITION)[:, unit_rows, :],
-                )
-                h2_words = h2_raw[:].bitcast(F32)
-                h2_grouped = work.tile([P, PASSES1 * UNIT * PACK], BF16, align_bytes=64)
-                h2_grouped_words = (
-                    h2_grouped[:].bitcast(F32).rearrange("p (g b u) -> p g b u", g=PASSES1, u=2)
-                )
-                for j in range(BLOCKS):
-                    flipped = psum.tile([P, 2 * PASSES1, P], F32, tag="flipped")
-                    for a in range(2 * PASSES1):
-                        first = j * WORDS + a * P
-                        nc.tensor.transpose(
-                            flipped[:, a, :], h2_words[:, first : first + P], ident_f32[:]
-                        )
-                    nc.scalar.copy(
-                        out=h2_grouped_words[:, :, j * P : (j + 1) * P, :],
-                        in_=flipped[:].rearrange("p (g u) b -> p g b u", u=2),
+        def flip_h2(u):
+            h2_words = h2_loaded[u][:].bitcast(F32)
+            h2_flipped[u] = []
+            for j in range(BLOCKS):
+                flipped = psum.tile([P, 2 * PASSES1, P], F32, tag="ring", bufs=RING)
+                for a in range(2 * PASSES1):
+                    first = j * WORDS + a * P
+                    nc.tensor.transpose(
+                        flipped[:, a, :], h2_words[:, first : first + P], ident_f32[:]
                     )
-                h2_codes = work.tile([P, PASSES1 * UNIT], U32, align_bytes=64)
-                h2_scales = work.tile([P, PASSES1 * UNIT], U8, align_bytes=64)
-                quantise(h2_codes[:], h2_scales[:], h2_grouped[:])
+                h2_flipped[u].append(flipped)
 
-                h_tiles = work.tile([P, H_TILES, UNIT], BF16)
-                for m in range(H_TILES):
-                    acc1 = psum.tile([P, UNIT], F32, tag="acc1")
-                    for g in range(PASSES1):
-                        w_cols = slice(g * K2 + m * P, g * K2 + (m + 1) * P)
-                        x_cols = slice(g * UNIT, (g + 1) * UNIT)
-                        nc.tensor.matmul_mx(
-                            out=acc1[:],
-                            lhsT=w3_codes[:, w_cols].bitcast(FP8X4),
-                            lhsT_scale=w3_scales[:, w_cols],
-                            rhs=h2_codes[:, x_cols].bitcast(FP8X4),
-                            rhs_scale=h2_scales[:, x_cols],
-                            start=(g == 0),
-                            stop=(g == PASSES1 - 1),
-                        )
-                    b3_col = ROW_B3 + e * H_TILES + m
-                    nc.scalar.activation(
-                        out=h_tiles[:, m, :],
-                        in_=acc1[:],
-                        func=ACT.Silu,
-                        bias=cols[:, b3_col : b3_col + 1],
-                        scale=1.0,
-                    )
-                h_grouped = work.tile([P, UNIT, PACK], BF16, align_bytes=64)
-                regroup(h_grouped[:], h_tiles[:])
-                h_codes = work.tile([P, UNIT], U32, align_bytes=64)
-                h_scales = work.tile([P, UNIT], U8, align_bytes=64)
-                quantise(h_codes[:], h_scales[:], h_grouped[:].rearrange("p b t -> p (b t)"))
+        def quantise_h2(u):
+            h2_grouped = work.tile([P, PASSES1 * UNIT * PACK], BF16, align_bytes=64)
+            h2_grouped_words = (
+                h2_grouped[:].bitcast(F32).rearrange("p (g b u) -> p g b u", g=PASSES1, u=2)
+            )
+            for j in range(BLOCKS):
+                nc.scalar.copy(
+                    out=h2_grouped_words[:, :, j * P : (j + 1) * P, :],
+                    in_=h2_flipped[u][j][:].rearrange("p (g u) b -> p g b u", u=2),
+                )
+            h2_codes = work.tile([P, PASSES1 * UNIT], U32, align_bytes=64)
+            h2_scales = work.tile([P, PASSES1 * UNIT], U8, align_bytes=64)
+            quantise(h2_codes[:], h2_scales[:], h2_grouped[:])
+            h2_quantised[u] = (h2_codes, h2_scales)
 
-                heads_t = []
-                for head in range(HEADS):
-                    acc2 = psum.tile([P, UNIT], F32, tag="acc2")
-                    w_cols = slice(head * STATE, (head + 1) * STATE)
+        def stage1(u):
+            e = u // UNITS
+            w3_codes, w3_scales = stage1_weights[e]
+            h2_codes, h2_scales = h2_quantised[u]
+            h_tiles = work.tile([P, H_TILES, UNIT], BF16)
+            for m in range(H_TILES):
+                acc1 = psum.tile([P, UNIT], F32, tag="ring", bufs=RING)
+                for g in range(PASSES1):
+                    w_cols = slice(g * K2 + m * P, g * K2 + (m + 1) * P)
+                    x_cols = slice(g * UNIT, (g + 1) * UNIT)
                     nc.tensor.matmul_mx(
-                        out=acc2[:],
-                        lhsT=w2_codes[:, w_cols].bitcast(FP8X4),
-                        lhsT_scale=w2_scales[:, w_cols],
-                        rhs=h_codes[:].bitcast(FP8X4),
-                        rhs_scale=h_scales[:],
-                        start=True,
-                        stop=True,
+                        out=acc1[:],
+                        lhsT=w3_codes[:, w_cols].bitcast(FP8X4),
+                        lhsT_scale=w3_scales[:, w_cols],
+                        rhs=h2_codes[:, x_cols].bitcast(FP8X4),
+                        rhs_scale=h2_scales[:, x_cols],
+                        start=(g == 0),
+                        stop=(g == PASSES1 - 1),
                     )
-                    heads_t.append(acc2)
-
-                mu_t = work.tile([P, UNIT], F32)
+                b3_col = ROW_B3 + e * H_TILES + m
                 nc.scalar.activation(
-                    out=mu_t[:],
-                    in_=heads_t[0][:],
-                    func=ACT.Identity,
-                    bias=cols[:, ROW_BMU + e : ROW_BMU + e + 1],
+                    out=h_tiles[:, m, :],
+                    in_=acc1[:],
+                    func=ACT.Silu,
+                    bias=cols[:, b3_col : b3_col + 1],
                     scale=1.0,
                 )
-                sigma_t = work.tile([P, UNIT], F32)
-                nc.scalar.activation(
-                    out=sigma_t[:],
-                    in_=heads_t[1][:],
-                    func=ACT.Tanh,
-                    bias=tanh_bias[:, e : e + 1],
-                    scale=0.5,
-                )
-                nc.vector.tensor_scalar(
-                    out=sigma_t[:],
-                    in0=sigma_t[:],
-                    scalar1=sigma_scale[:, 0:1],
-                    scalar2=sigma_shift[:, 0:1],
-                    op0=ALU.mult,
-                    op1=ALU.add,
-                )
+            h_plain[u] = h_tiles
 
-                mu_back = psum.tile([P, BLOCKS, STATE], F32, tag="back")
-                for j in range(BLOCKS):
-                    nc.tensor.transpose(mu_back[:, j, :], mu_t[:, j * P : (j + 1) * P], ident_f32[:])
-                mu_out = results.tile([P, BLOCKS, STATE], F32)
-                nc.vector.tensor_tensor(
-                    out=mu_out[:], in0=mu_back[:], in1=state_sb[:, unit_rows, :], op=ALU.add
-                )
-                nc.sync.dma_start(
-                    out=out_0[e].rearrange("(p j) s -> p j s", j=ROWS_PER_PARTITION)[:, unit_rows, :],
-                    in_=mu_out[:],
-                )
+        def regroup_h(u):
+            h_grouped = work.tile([P, UNIT, PACK], BF16, align_bytes=64)
+            regroup(h_grouped[:], h_plain[u][:])
+            h_regrouped[u] = h_grouped
 
-                sigma_back = psum.tile([P, BLOCKS, STATE], F32, tag="back")
-                for j in range(BLOCKS):
-                    nc.tensor.transpose(
-                        sigma_back[:, j, :], sigma_t[:, j * P : (j + 1) * P], ident_f32[:]
-                    )
-                sigma_out = results.tile([P, BLOCKS, STATE], F32)
-                nc.scalar.copy(out=sigma_out[:], in_=sigma_back[:])
-                nc.sync.dma_start(
-                    out=out_1[e].rearrange("(p j) s -> p j s", j=ROWS_PER_PARTITION)[:, unit_rows, :],
-                    in_=sigma_out[:],
+        def quantise_h(u):
+            h_codes = work.tile([P, UNIT], U32, align_bytes=64)
+            h_scales = work.tile([P, UNIT], U8, align_bytes=64)
+            quantise(h_codes[:], h_scales[:], h_regrouped[u][:].rearrange("p b t -> p (b t)"))
+            h_quantised[u] = (h_codes, h_scales)
+
+        def stage2(u):
+            e = u // UNITS
+            w2_codes, w2_scales = stage2_weights[e]
+            h_codes, h_scales = h_quantised[u]
+            products = []
+            for head in range(HEADS):
+                acc2 = psum.tile([P, UNIT], F32, tag="acc2")
+                w_cols = slice(head * STATE, (head + 1) * STATE)
+                nc.tensor.matmul_mx(
+                    out=acc2[:],
+                    lhsT=w2_codes[:, w_cols].bitcast(FP8X4),
+                    lhsT_scale=w2_scales[:, w_cols],
+                    rhs=h_codes[:].bitcast(FP8X4),
+                    rhs_scale=h_scales[:],
+                    start=True,
+                    stop=True,
                 )
+                products.append(acc2)
+            mu_t = work.tile([P, UNIT], F32)
+            nc.scalar.activation(
+                out=mu_t[:],
+                in_=products[0][:],
+                func=ACT.Identity,
+                bias=cols[:, ROW_BMU + e : ROW_BMU + e + 1],
+                scale=1.0,
+            )
+            mu_transposed[u] = mu_t
+            sigma_t = work.tile([P, UNIT], F32)
+            nc.scalar.activation(
+                out=sigma_t[:],
+                in_=products[1][:],
+                func=ACT.Tanh,
+                bias=tanh_bias[:, e : e + 1],
+                scale=0.5,
+            )
+            sigma_transposed[u] = sigma_t
+
+        def scale_sigma(u):
+            sigma_t = sigma_transposed[u]
+            nc.vector.tensor_scalar(
+                out=sigma_t[:],
+                in0=sigma_t[:],
+                scalar1=sigma_scale[:, 0:1],
+                scalar2=sigma_shift[:, 0:1],
+                op0=ALU.mult,
+                op1=ALU.add,
+            )
+
+        def flip_back(transposed):
+            back = psum.tile([P, BLOCKS, STATE], F32, tag="back")
+            for j in range(BLOCKS):
+                nc.tensor.transpose(back[:, j, :], transposed[:, j * P : (j + 1) * P], ident_f32[:])
+            return back
+
+        def flip_mu(u):
+            mu_banks[u] = flip_back(mu_transposed[u])
+
+        def flip_sigma(u):
+            sigma_banks[u] = flip_back(sigma_transposed[u])
+
+        def store_mu(u):
+            n = u % UNITS
+            mu_out = results.tile([P, BLOCKS, STATE], F32)
+            nc.vector.tensor_tensor(
+                out=mu_out[:],
+                in0=mu_banks[u][:],
+                in1=state_sb[:, BLOCKS * n : BLOCKS * (n + 1), :],
+                op=ALU.add,
+            )
+            nc.sync.dma_start(out=batch_rows(out_0, u), in_=mu_out[:])
+
+        def store_sigma(u):
+            sigma_out = results.tile([P, BLOCKS, STATE], F32)
+            nc.scalar.copy(out=sigma_out[:], in_=sigma_banks[u][:])
+            nc.sync.dma_start(out=batch_rows(out_1, u), in_=sigma_out[:])
+
+        def for_unit(stage, u):
+            if 0 <= u < N_UNITS:
+                stage(u)
+
+        def for_member(stage, first_unit):
+            if first_unit % UNITS == 0 and 0 <= first_unit < N_UNITS:
+                stage(first_unit // UNITS)
+
+        for s in range(-4, N_UNITS + 2):
+            for_member(load_weights, s + 4)
+            for_unit(load_h2, s + 3)
+            for_member(regroup_w3, s + 2)
+            for_member(quantise_weights, s + 1)
+            for_unit(quantise_h2, s + 1)
+            for_unit(stage1, s)
+            for_unit(stage2, s - 1)
+            for_unit(flip_sigma, s - 2)
+            for_unit(flip_h2, s + 2)
+            for_unit(store_sigma, s - 2)
+            for_unit(flip_mu, s - 1)
+            for_unit(regroup_h, s)
+            for_unit(store_mu, s - 1)
+            for_unit(quantise_h, s)
+            for_unit(scale_sigma, s - 1)

@@ -29,7 +29,8 @@ UNITS = BATCH // UNIT
 N_UNITS = MEMBERS * UNITS
 WORDS = K1 // 2
 HEADS = 2
-RING = 4
+BANKS = 8
+PAIR = 2
 RUN = 4
 
 ROW_B3 = 0
@@ -57,11 +58,11 @@ def tile_ensembledynamicmodel_pa_t_kernel(
 
     with ExitStack() as ctx:
         consts = ctx.enter_context(tc.tile_pool(name="consts", bufs=1))
-        h2_pool = ctx.enter_context(tc.tile_pool(name="h2_pool", bufs=4))
+        h2_pool = ctx.enter_context(tc.tile_pool(name="h2_pool", bufs=5))
         weights = ctx.enter_context(tc.tile_pool(name="weights", bufs=2))
         work = ctx.enter_context(tc.tile_pool(name="work", bufs=3))
         results = ctx.enter_context(tc.tile_pool(name="results", bufs=3))
-        psum = ctx.enter_context(tc.psum_pool(name="psum", bufs=2))
+        psum = ctx.enter_context(tc.psum_pool(name="psum", bufs=BANKS))
         ctx.enter_context(tc.manual_schedule())
 
         ident_f32 = consts.tile([P, P], F32)
@@ -87,7 +88,7 @@ def tile_ensembledynamicmodel_pa_t_kernel(
             out=state_sb[:], in_=state.rearrange("(p j) s -> p j s", j=ROWS_PER_PARTITION)
         )
 
-        cols_ps = psum.tile([P, P], BF16, tag="back")
+        cols_ps = psum.tile([P, P], BF16, tag="bank")
         nc.tensor.transpose(cols_ps[:], rows[:], ident_bf16[:])
         cols = consts.tile([P, P], F32)
         nc.vector.tensor_copy(out=cols[:], in_=cols_ps[:])
@@ -117,7 +118,7 @@ def tile_ensembledynamicmodel_pa_t_kernel(
         nc.scalar.activation(out=table_warmer[:], in_=sigma_shift[:], func=ACT.Silu)
 
         raw_weights, grouped_w3, stage1_weights, stage2_weights = {}, {}, {}, {}
-        h2_loaded, h2_flipped, h2_quantised = {}, {}, {}
+        h2_loaded, h2_regrouped, h2_quantised = {}, {}, {}
         h_plain, h_regrouped, h_quantised = {}, {}, {}
         mu_transposed, sigma_transposed, mu_banks, sigma_banks = {}, {}, {}, {}
 
@@ -165,40 +166,41 @@ def tile_ensembledynamicmodel_pa_t_kernel(
             )
             h2_loaded[u] = h2_raw
 
-        def flip_h2(u):
+        def transpose_h2(u, first_block):
             h2_words = h2_loaded[u][:].bitcast(F32)
-            h2_flipped[u] = []
-            for j in range(BLOCKS):
-                flipped = psum.tile([P, 2 * PASSES1, P], F32, tag="ring", bufs=RING)
+            if first_block == 0:
+                h2_grouped = work.tile([P, PASSES1 * UNIT * PACK], BF16, align_bytes=64)
+                h2_regrouped[u] = h2_grouped
+            h2_grouped_words = (
+                h2_regrouped[u][:].bitcast(F32).rearrange("p (g b u) -> p g b u", g=PASSES1, u=2)
+            )
+            for j in range(first_block, first_block + PAIR):
+                flipped = psum.tile([P, 2 * PASSES1, P], F32, tag="bank")
                 for a in range(2 * PASSES1):
                     first = j * WORDS + a * P
                     nc.tensor.transpose(
                         flipped[:, a, :], h2_words[:, first : first + P], ident_f32[:]
                     )
-                h2_flipped[u].append(flipped)
-
-        def quantise_h2(u):
-            h2_grouped = work.tile([P, PASSES1 * UNIT * PACK], BF16, align_bytes=64)
-            h2_grouped_words = (
-                h2_grouped[:].bitcast(F32).rearrange("p (g b u) -> p g b u", g=PASSES1, u=2)
-            )
-            for j in range(BLOCKS):
                 nc.scalar.copy(
                     out=h2_grouped_words[:, :, j * P : (j + 1) * P, :],
-                    in_=h2_flipped[u][j][:].rearrange("p (g u) b -> p g b u", u=2),
+                    in_=flipped[:].rearrange("p (g u) b -> p g b u", u=2),
                 )
+
+        def quantise_h2(u):
             h2_codes = work.tile([P, PASSES1 * UNIT], U32, align_bytes=64)
             h2_scales = work.tile([P, PASSES1 * UNIT], U8, align_bytes=64)
-            quantise(h2_codes[:], h2_scales[:], h2_grouped[:])
+            quantise(h2_codes[:], h2_scales[:], h2_regrouped[u][:])
             h2_quantised[u] = (h2_codes, h2_scales)
 
-        def stage1(u):
+        def stage1(u, first_tile):
             e = u // UNITS
             w3_codes, w3_scales = stage1_weights[e]
             h2_codes, h2_scales = h2_quantised[u]
-            h_tiles = work.tile([P, H_TILES, UNIT], BF16)
-            for m in range(H_TILES):
-                acc1 = psum.tile([P, UNIT], F32, tag="ring", bufs=RING)
+            if first_tile == 0:
+                h_tiles = work.tile([P, H_TILES, UNIT], BF16)
+                h_plain[u] = h_tiles
+            for m in range(first_tile, first_tile + PAIR):
+                acc1 = psum.tile([P, UNIT], F32, tag="bank")
                 for g in range(PASSES1):
                     w_cols = slice(g * K2 + m * P, g * K2 + (m + 1) * P)
                     x_cols = slice(g * UNIT, (g + 1) * UNIT)
@@ -213,13 +215,12 @@ def tile_ensembledynamicmodel_pa_t_kernel(
                     )
                 b3_col = ROW_B3 + e * H_TILES + m
                 nc.scalar.activation(
-                    out=h_tiles[:, m, :],
+                    out=h_plain[u][:, m, :],
                     in_=acc1[:],
                     func=ACT.Silu,
                     bias=cols[:, b3_col : b3_col + 1],
                     scale=1.0,
                 )
-            h_plain[u] = h_tiles
 
         def regroup_h(u):
             h_grouped = work.tile([P, UNIT, PACK], BF16, align_bytes=64)
@@ -238,7 +239,7 @@ def tile_ensembledynamicmodel_pa_t_kernel(
             h_codes, h_scales = h_quantised[u]
             products = []
             for head in range(HEADS):
-                acc2 = psum.tile([P, UNIT], F32, tag="acc2")
+                acc2 = psum.tile([P, UNIT], F32, tag="bank")
                 w_cols = slice(head * STATE, (head + 1) * STATE)
                 nc.tensor.matmul_mx(
                     out=acc2[:],
@@ -281,7 +282,7 @@ def tile_ensembledynamicmodel_pa_t_kernel(
             )
 
         def flip_back(transposed):
-            back = psum.tile([P, BLOCKS, STATE], F32, tag="back")
+            back = psum.tile([P, BLOCKS, STATE], F32, tag="bank")
             for j in range(BLOCKS):
                 nc.tensor.transpose(back[:, j, :], transposed[:, j * P : (j + 1) * P], ident_f32[:])
             return back
@@ -308,27 +309,28 @@ def tile_ensembledynamicmodel_pa_t_kernel(
             nc.scalar.copy(out=sigma_out[:], in_=sigma_banks[u][:])
             nc.sync.dma_start(out=batch_rows(out_1, u), in_=sigma_out[:])
 
-        def for_unit(stage, u):
+        def for_unit(stage, u, *args):
             if 0 <= u < N_UNITS:
-                stage(u)
+                stage(u, *args)
 
         def for_member(stage, first_unit):
             if first_unit % UNITS == 0 and 0 <= first_unit < N_UNITS:
                 stage(first_unit // UNITS)
 
         for s in range(-4, N_UNITS + 2):
+            for_unit(load_h2, s + 4)
             for_member(load_weights, s + 4)
-            for_unit(load_h2, s + 3)
             for_member(regroup_w3, s + 2)
             for_member(quantise_weights, s + 1)
-            for_unit(quantise_h2, s + 1)
-            for_unit(stage1, s)
+            for first in range(0, BLOCKS, PAIR):
+                for_unit(stage1, s, first)
+                for_unit(transpose_h2, s + 2, first)
+            for_unit(regroup_h, s)
+            for_unit(quantise_h2, s + 2)
             for_unit(stage2, s - 1)
             for_unit(flip_sigma, s - 2)
-            for_unit(flip_h2, s + 2)
+            for_unit(flip_mu, s - 2)
             for_unit(store_sigma, s - 2)
-            for_unit(flip_mu, s - 1)
-            for_unit(regroup_h, s)
-            for_unit(store_mu, s - 1)
+            for_unit(store_mu, s - 2)
             for_unit(quantise_h, s)
             for_unit(scale_sigma, s - 1)

@@ -322,15 +322,16 @@ def tile_ensembledynamicmodel_pa_t_kernel(
             for_member(load_weights, s + 4)
             for_member(regroup_w3, s + 2)
             for_member(quantise_weights, s + 1)
-            for first in range(0, BLOCKS, PAIR):
-                for_unit(stage1, s, first)
-                for_unit(transpose_h2, s + 2, first)
-            for_unit(regroup_h, s)
-            for_unit(quantise_h2, s + 2)
+            for_unit(stage1, s, 0)
+            for_unit(transpose_h2, s + 2, 0)
+            for_unit(stage1, s, PAIR)
             for_unit(stage2, s - 1)
+            for_unit(transpose_h2, s + 2, PAIR)
             for_unit(flip_sigma, s - 2)
             for_unit(flip_mu, s - 2)
             for_unit(store_sigma, s - 2)
+            for_unit(regroup_h, s)
             for_unit(store_mu, s - 2)
             for_unit(quantise_h, s)
             for_unit(scale_sigma, s - 1)
+            for_unit(quantise_h2, s + 2)

@@ -31,6 +31,7 @@ WORDS = K1 // 2
 HEADS = 2
 BANKS = 8
 PAIR = 2
+SIGMA_TO_VECTOR = 3
 RUN = 4
 
 ROW_B3 = 0
@@ -117,7 +118,7 @@ def tile_ensembledynamicmodel_pa_t_kernel(
         table_warmer = consts.tile([P, 1], F32)
         nc.scalar.activation(out=table_warmer[:], in_=sigma_shift[:], func=ACT.Silu)
 
-        raw_weights, grouped_w3, stage1_weights, stage2_weights = {}, {}, {}, {}
+        raw_w3, raw_w2, grouped_w3, grouped_w2, stage1_weights, stage2_weights = {}, {}, {}, {}, {}, {}
         h2_loaded, h2_regrouped, h2_quantised = {}, {}, {}
         h_plain, h_regrouped, h_quantised = {}, {}, {}
         mu_transposed, sigma_transposed, mu_banks, sigma_banks = {}, {}, {}, {}
@@ -127,43 +128,56 @@ def tile_ensembledynamicmodel_pa_t_kernel(
             by_partition = dram[e].rearrange("(p j) x -> p j x", j=ROWS_PER_PARTITION)
             return by_partition[:, BLOCKS * n : BLOCKS * (n + 1), :]
 
-        def load_weights(e):
+        def load_w3(e):
             w3_raw = weights.tile([P, 2 * PASSES1, 2 * K2], BF16)
-            nc.sync.dma_start(
-                out=w3_raw[:], in_=W3[e].rearrange("(a q r) c -> q a (r c)", q=P, r=2)
-            )
+            for g in range(PASSES1):
+                nc.sync.dma_start(
+                    out=w3_raw[:, 2 * g : 2 * (g + 1), :],
+                    in_=W3[e, K_PASS * g : K_PASS * (g + 1), :].rearrange(
+                        "(a q r) c -> q a (r c)", q=P, r=2
+                    ),
+                )
+            raw_w3[e] = w3_raw
+
+        def load_w2(e):
             w2_raw = weights.tile([P, HEADS, PACK, STATE], BF16)
             nc.sync.dma_start(out=w2_raw[:, 0], in_=Wmu[e].rearrange("(t p) s -> p t s", p=P))
             nc.sync.dma_start(out=w2_raw[:, 1], in_=Wsig[e].rearrange("(t p) s -> p t s", p=P))
-            raw_weights[e] = (w3_raw, w2_raw)
+            raw_w2[e] = w2_raw
 
         def regroup_w3(e):
-            w3_raw = raw_weights[e][0]
-            w3_rows = w3_raw[:].rearrange("p a (r c) -> p (a r) c", r=2)
+            w3_rows = raw_w3[e][:].rearrange("p a (r c) -> p (a r) c", r=2)
             w3_grouped = weights.tile([P, PASSES1, K2, PACK], BF16, align_bytes=64)
             for g in range(PASSES1):
                 regroup(w3_grouped[:, g], w3_rows[:, PACK * g : PACK * (g + 1), :])
             grouped_w3[e] = w3_grouped
 
-        def quantise_weights(e):
-            w2_raw = raw_weights[e][1]
-            w2_grouped = weights.tile([P, HEADS, STATE, PACK], BF16, align_bytes=64)
-            for head in range(HEADS):
-                regroup(w2_grouped[:, head], w2_raw[:, head])
+        def quantise_w3(e):
             w3_codes = weights.tile([P, PASSES1 * K2], U32, align_bytes=64)
             w3_scales = weights.tile([P, PASSES1 * K2], U8, align_bytes=64)
             quantise(w3_codes[:], w3_scales[:], grouped_w3[e][:].rearrange("p g c t -> p (g c t)"))
             stage1_weights[e] = (w3_codes, w3_scales)
+
+        def regroup_w2(e):
+            w2_grouped = weights.tile([P, HEADS, STATE, PACK], BF16, align_bytes=64)
+            for head in range(HEADS):
+                regroup(w2_grouped[:, head], raw_w2[e][:, head])
+            grouped_w2[e] = w2_grouped
+
+        def quantise_w2(e):
             w2_codes = weights.tile([P, HEADS * STATE], U32, align_bytes=64)
             w2_scales = weights.tile([P, HEADS * STATE], U8, align_bytes=64)
-            quantise(w2_codes[:], w2_scales[:], w2_grouped[:].rearrange("p w s t -> p (w s t)"))
+            quantise(w2_codes[:], w2_scales[:], grouped_w2[e][:].rearrange("p w s t -> p (w s t)"))
             stage2_weights[e] = (w2_codes, w2_scales)
 
         def load_h2(u):
             h2_raw = h2_pool.tile([P, BLOCKS * K1], BF16)
-            nc.sync.dma_start(
-                out=h2_raw[:].rearrange("p (j k) -> p j k", j=BLOCKS), in_=batch_rows(h2, u)
-            )
+            h2_blocks = h2_raw[:].rearrange("p (j k) -> p j k", j=BLOCKS)
+            for first in range(0, BLOCKS, PAIR):
+                nc.sync.dma_start(
+                    out=h2_blocks[:, first : first + PAIR, :],
+                    in_=batch_rows(h2, u)[:, first : first + PAIR, :],
+                )
             h2_loaded[u] = h2_raw
 
         def transpose_h2(u, first_block):
@@ -306,7 +320,10 @@ def tile_ensembledynamicmodel_pa_t_kernel(
 
         def store_sigma(u):
             sigma_out = results.tile([P, BLOCKS, STATE], F32)
-            nc.scalar.copy(out=sigma_out[:], in_=sigma_banks[u][:])
+            if u % SIGMA_TO_VECTOR == SIGMA_TO_VECTOR - 1:
+                nc.vector.tensor_copy(out=sigma_out[:], in_=sigma_banks[u][:])
+            else:
+                nc.scalar.copy(out=sigma_out[:], in_=sigma_banks[u][:])
             nc.sync.dma_start(out=batch_rows(out_1, u), in_=sigma_out[:])
 
         def for_unit(stage, u, *args):
@@ -319,19 +336,21 @@ def tile_ensembledynamicmodel_pa_t_kernel(
 
         for s in range(-4, N_UNITS + 2):
             for_unit(load_h2, s + 4)
-            for_member(load_weights, s + 4)
+            for_member(load_w3, s + 4)
+            for_member(load_w2, s + 3)
             for_member(regroup_w3, s + 2)
-            for_member(quantise_weights, s + 1)
-            for_unit(stage1, s, 0)
-            for_unit(transpose_h2, s + 2, 0)
-            for_unit(stage1, s, PAIR)
+            for_member(quantise_w3, s + 1)
+            for_member(regroup_w2, s + 1)
+            for first in range(0, BLOCKS, PAIR):
+                for_unit(stage1, s, first)
+                for_unit(transpose_h2, s + 2, first)
+            for_unit(regroup_h, s)
+            for_unit(quantise_h2, s + 2)
+            for_unit(quantise_h, s)
+            for_member(quantise_w2, s + 1)
             for_unit(stage2, s - 1)
-            for_unit(transpose_h2, s + 2, PAIR)
+            for_unit(scale_sigma, s - 1)
             for_unit(flip_sigma, s - 2)
             for_unit(flip_mu, s - 2)
             for_unit(store_sigma, s - 2)
-            for_unit(regroup_h, s)
             for_unit(store_mu, s - 2)
-            for_unit(quantise_h, s)
-            for_unit(scale_sigma, s - 1)
-            for_unit(quantise_h2, s + 2)

@@ -31,7 +31,6 @@ WORDS = K1 // 2
 HEADS = 2
 BANKS = 8
 PAIR = 2
-SIGMA_TO_VECTOR = 3
 RUN = 4
 
 ROW_B3 = 0
@@ -60,63 +59,18 @@ def tile_ensembledynamicmodel_pa_t_kernel(
     with ExitStack() as ctx:
         consts = ctx.enter_context(tc.tile_pool(name="consts", bufs=1))
         h2_pool = ctx.enter_context(tc.tile_pool(name="h2_pool", bufs=5))
-        weights = ctx.enter_context(tc.tile_pool(name="weights", bufs=2))
+        weights = ctx.enter_context(tc.tile_pool(name="weights", bufs=3))
         work = ctx.enter_context(tc.tile_pool(name="work", bufs=3))
         results = ctx.enter_context(tc.tile_pool(name="results", bufs=3))
         psum = ctx.enter_context(tc.psum_pool(name="psum", bufs=BANKS))
         ctx.enter_context(tc.manual_schedule())
 
-        ident_f32 = consts.tile([P, P], F32)
-        make_identity(nc, ident_f32[:])
-        ident_bf16 = consts.tile([P, P], BF16)
-        make_identity(nc, ident_bf16[:])
-
-        rows = consts.tile([P, P], BF16)
-        nc.vector.memset(rows[:], 0.0)
-        nc.scalar.dma_start(
-            out=rows[ROW_B3:ROW_BMU, :], in_=b3.rearrange("e (t p) -> (e t) p", p=P)
-        )
-        nc.scalar.dma_start(out=rows[ROW_BMU:ROW_BSIG, :], in_=bmu)
-        nc.scalar.dma_start(out=rows[ROW_BSIG:ROW_MAX, :], in_=bsig)
-        nc.scalar.dma_start(
-            out=rows[ROW_MAX : ROW_MAX + 1, :], in_=max_logstd.rearrange("(o s) -> o s", o=1)
-        )
-        nc.scalar.dma_start(
-            out=rows[ROW_MIN : ROW_MIN + 1, :], in_=min_logstd.rearrange("(o s) -> o s", o=1)
-        )
-        state_sb = consts.tile([P, ROWS_PER_PARTITION, STATE], BF16)
-        nc.scalar.dma_start(
-            out=state_sb[:], in_=state.rearrange("(p j) s -> p j s", j=ROWS_PER_PARTITION)
-        )
-
-        cols_ps = psum.tile([P, P], BF16, tag="bank")
-        nc.tensor.transpose(cols_ps[:], rows[:], ident_bf16[:])
         cols = consts.tile([P, P], F32)
-        nc.vector.tensor_copy(out=cols[:], in_=cols_ps[:])
-
         tanh_bias = consts.tile([P, MEMBERS], F32)
-        nc.vector.tensor_scalar(
-            out=tanh_bias[:],
-            in0=cols[:, ROW_BSIG:ROW_MAX],
-            scalar1=cols[:, ROW_MAX : ROW_MAX + 1],
-            scalar2=0.5,
-            op0=ALU.subtract,
-            op1=ALU.mult,
-        )
         exp_bounds = consts.tile([P, 2], F32)
-        nc.scalar.activation(out=exp_bounds[:], in_=cols[:, ROW_MAX : ROW_MIN + 1], func=ACT.Exp)
         sigma_scale = consts.tile([P, 1], F32)
-        nc.scalar.mul(out=sigma_scale[:], in_=exp_bounds[:, 0:1], mul=0.5)
         sigma_shift = consts.tile([P, 1], F32)
-        nc.scalar.activation(
-            out=sigma_shift[:],
-            in_=exp_bounds[:, 1:2],
-            func=ACT.Identity,
-            bias=sigma_scale[:, 0:1],
-            scale=1.0,
-        )
         table_warmer = consts.tile([P, 1], F32)
-        nc.scalar.activation(out=table_warmer[:], in_=sigma_shift[:], func=ACT.Silu)
 
         raw_w3, raw_w2, grouped_w3, grouped_w2, stage1_weights, stage2_weights = {}, {}, {}, {}, {}, {}
         h2_loaded, h2_regrouped, h2_quantised = {}, {}, {}
@@ -148,20 +102,37 @@ def tile_ensembledynamicmodel_pa_t_kernel(
         def regroup_w3(e):
             w3_rows = raw_w3[e][:].rearrange("p a (r c) -> p (a r) c", r=2)
             w3_grouped = weights.tile([P, PASSES1, K2, PACK], BF16, align_bytes=64)
-            for g in range(PASSES1):
-                regroup(w3_grouped[:, g], w3_rows[:, PACK * g : PACK * (g + 1), :])
+            if e == 0:
+                for g in range(PASSES1):
+                    regroup(w3_grouped[:, g], w3_rows[:, PACK * g : PACK * (g + 1), :])
+            else:
+                nc.vector.tensor_copy(
+                    out=w3_grouped[:].rearrange("p g (c i) t -> p g c t i", i=RUN),
+                    in_=w3_rows.rearrange("p (g t) (c i) -> p g c t i", t=PACK, i=RUN),
+                )
             grouped_w3[e] = w3_grouped
 
         def quantise_w3(e):
             w3_codes = weights.tile([P, PASSES1 * K2], U32, align_bytes=64)
             w3_scales = weights.tile([P, PASSES1 * K2], U8, align_bytes=64)
-            quantise(w3_codes[:], w3_scales[:], grouped_w3[e][:].rearrange("p g c t -> p (g c t)"))
+            if e == 0:
+                for g in range(PASSES1):
+                    cols_g = slice(g * K2, (g + 1) * K2)
+                    quantise(
+                        w3_codes[:, cols_g],
+                        w3_scales[:, cols_g],
+                        grouped_w3[e][:, g].rearrange("p c t -> p (c t)"),
+                    )
+            else:
+                quantise(w3_codes[:], w3_scales[:], grouped_w3[e][:].rearrange("p g c t -> p (g c t)"))
             stage1_weights[e] = (w3_codes, w3_scales)
 
         def regroup_w2(e):
             w2_grouped = weights.tile([P, HEADS, STATE, PACK], BF16, align_bytes=64)
-            for head in range(HEADS):
-                regroup(w2_grouped[:, head], raw_w2[e][:, head])
+            nc.vector.tensor_copy(
+                out=w2_grouped[:].rearrange("p w (s i) t -> p w s t i", i=RUN),
+                in_=raw_w2[e][:].rearrange("p w t (s i) -> p w s t i", i=RUN),
+            )
             grouped_w2[e] = w2_grouped
 
         def quantise_w2(e):
@@ -320,11 +291,65 @@ def tile_ensembledynamicmodel_pa_t_kernel(
 
         def store_sigma(u):
             sigma_out = results.tile([P, BLOCKS, STATE], F32)
-            if u % SIGMA_TO_VECTOR == SIGMA_TO_VECTOR - 1:
-                nc.vector.tensor_copy(out=sigma_out[:], in_=sigma_banks[u][:])
-            else:
-                nc.scalar.copy(out=sigma_out[:], in_=sigma_banks[u][:])
+            nc.scalar.copy(out=sigma_out[:], in_=sigma_banks[u][:])
             nc.sync.dma_start(out=batch_rows(out_1, u), in_=sigma_out[:])
+
+        load_w3(0)
+
+        ident_f32 = consts.tile([P, P], F32)
+        make_identity(nc, ident_f32[:])
+        ident_bf16 = consts.tile([P, P], BF16)
+        make_identity(nc, ident_bf16[:])
+
+        rows = consts.tile([P, P], BF16)
+        nc.vector.memset(rows[:], 0.0)
+        nc.scalar.activation(out=table_warmer[:], in_=rows[:, 0:1], func=ACT.Exp)
+        nc.scalar.dma_start(
+            out=rows[ROW_B3:ROW_BMU, :], in_=b3.rearrange("e (t p) -> (e t) p", p=P)
+        )
+        nc.scalar.dma_start(out=rows[ROW_BMU:ROW_BSIG, :], in_=bmu)
+        nc.scalar.dma_start(out=rows[ROW_BSIG:ROW_MAX, :], in_=bsig)
+        nc.scalar.dma_start(
+            out=rows[ROW_MAX : ROW_MAX + 1, :], in_=max_logstd.rearrange("(o s) -> o s", o=1)
+        )
+        nc.scalar.dma_start(
+            out=rows[ROW_MIN : ROW_MIN + 1, :], in_=min_logstd.rearrange("(o s) -> o s", o=1)
+        )
+        load_h2(0)
+        load_w3(1)
+        load_h2(1)
+        state_sb = consts.tile([P, ROWS_PER_PARTITION, STATE], BF16)
+        nc.sync.dma_start(
+            out=state_sb[:], in_=state.rearrange("(p j) s -> p j s", j=ROWS_PER_PARTITION)
+        )
+
+        regroup_w3(0)
+        quantise_w3(0)
+
+        def small_vectors():
+            cols_ps = psum.tile([P, P], BF16, tag="bank")
+            nc.tensor.transpose(cols_ps[:], rows[:], ident_bf16[:])
+            nc.vector.tensor_copy(out=cols[:], in_=cols_ps[:])
+            nc.vector.tensor_scalar(
+                out=tanh_bias[:],
+                in0=cols[:, ROW_BSIG:ROW_MAX],
+                scalar1=cols[:, ROW_MAX : ROW_MAX + 1],
+                scalar2=0.5,
+                op0=ALU.subtract,
+                op1=ALU.mult,
+            )
+            nc.scalar.activation(
+                out=exp_bounds[:], in_=cols[:, ROW_MAX : ROW_MIN + 1], func=ACT.Exp
+            )
+            nc.scalar.mul(out=sigma_scale[:], in_=exp_bounds[:, 0:1], mul=0.5)
+            nc.scalar.activation(
+                out=sigma_shift[:],
+                in_=exp_bounds[:, 1:2],
+                func=ACT.Identity,
+                bias=sigma_scale[:, 0:1],
+                scale=1.0,
+            )
+            nc.scalar.activation(out=table_warmer[:], in_=sigma_shift[:], func=ACT.Silu)
 
         def for_unit(stage, u, *args):
             if 0 <= u < N_UNITS:
@@ -334,20 +359,23 @@ def tile_ensembledynamicmodel_pa_t_kernel(
             if first_unit % UNITS == 0 and 0 <= first_unit < N_UNITS:
                 stage(first_unit // UNITS)
 
-        for s in range(-4, N_UNITS + 2):
+        for s in range(-2, N_UNITS + 2):
             for_unit(load_h2, s + 4)
-            for_member(load_w3, s + 4)
-            for_member(load_w2, s + 3)
-            for_member(regroup_w3, s + 2)
-            for_member(quantise_w3, s + 1)
-            for_member(regroup_w2, s + 1)
+            for_member(load_w2, s + 2)
+            for_member(load_w3, s + 5)
+            for_member(regroup_w3, s + 3)
+            if s + 2 > 0:
+                for_member(quantise_w3, s + 2)
+            for_member(regroup_w2, s)
             for first in range(0, BLOCKS, PAIR):
                 for_unit(stage1, s, first)
                 for_unit(transpose_h2, s + 2, first)
+            if s == -2:
+                small_vectors()
             for_unit(regroup_h, s)
             for_unit(quantise_h2, s + 2)
             for_unit(quantise_h, s)
-            for_member(quantise_w2, s + 1)
+            for_member(quantise_w2, s)
             for_unit(stage2, s - 1)
             for_unit(scale_sigma, s - 1)
             for_unit(flip_sigma, s - 2)

@@ -23,15 +23,16 @@ K_PASS = P * PACK
 PASSES1 = K1 // K_PASS
 H_TILES = K2 // P
 ROWS_PER_PARTITION = BATCH // P
-UNIT = 512
-BLOCKS = UNIT // P
-UNITS = BATCH // UNIT
-N_UNITS = MEMBERS * UNITS
 WORDS = K1 // 2
 HEADS = 2
 BANKS = 8
-PAIR = 2
+BANK = 512
 RUN = 4
+
+BLOCKS_FIRST = (4,4)
+BLOCKS_MIDDLE = (4, 4)
+BLOCKS_LAST = (4,2,2)
+W2_GROUPS = ((0,), (1,), (2,), (3,), (4,), (5,), (6,))
 
 ROW_B3 = 0
 ROW_BMU = ROW_B3 + MEMBERS * H_TILES
@@ -42,10 +43,24 @@ ROW_MIN = ROW_MAX + 1
 FLOPS = 2 * MEMBERS * BATCH * (K1 * K2 + K2 * HEADS * STATE)
 
 
+def cut_into_units():
+    units = []
+    for e in range(MEMBERS):
+        blocks = BLOCKS_FIRST if e == 0 else BLOCKS_LAST if e == MEMBERS - 1 else BLOCKS_MIDDLE
+        first = 0
+        for n in blocks:
+            units.append((e, first, n))
+            first += n
+    return units
+
+
 def tile_ensembledynamicmodel_pa_t_kernel(
     tc, h2, W3, b3, Wmu, bmu, Wsig, bsig, max_logstd, min_logstd, state, out_0, out_1
 ):
     nc = tc.nc
+    units = cut_into_units()
+    first_unit = {e: [u[0] for u in units].index(e) for e in range(MEMBERS)}
+    group_of = {e: group for group in W2_GROUPS for e in group}
 
     def regroup(dst, src):
         nc.vector.tensor_copy(
@@ -61,16 +76,9 @@ def tile_ensembledynamicmodel_pa_t_kernel(
         h2_pool = ctx.enter_context(tc.tile_pool(name="h2_pool", bufs=5))
         weights = ctx.enter_context(tc.tile_pool(name="weights", bufs=3))
         work = ctx.enter_context(tc.tile_pool(name="work", bufs=3))
-        results = ctx.enter_context(tc.tile_pool(name="results", bufs=3))
+        results = ctx.enter_context(tc.tile_pool(name="results", bufs=6))
         psum = ctx.enter_context(tc.psum_pool(name="psum", bufs=BANKS))
         ctx.enter_context(tc.manual_schedule())
-
-        cols = consts.tile([P, P], F32)
-        tanh_bias = consts.tile([P, MEMBERS], F32)
-        exp_bounds = consts.tile([P, 2], F32)
-        sigma_scale = consts.tile([P, 1], F32)
-        sigma_shift = consts.tile([P, 1], F32)
-        table_warmer = consts.tile([P, 1], F32)
 
         raw_w3, raw_w2, grouped_w3, grouped_w2, stage1_weights, stage2_weights = {}, {}, {}, {}, {}, {}
         h2_loaded, h2_regrouped, h2_quantised = {}, {}, {}
@@ -78,88 +86,103 @@ def tile_ensembledynamicmodel_pa_t_kernel(
         mu_transposed, sigma_transposed, mu_banks, sigma_banks = {}, {}, {}, {}
 
         def batch_rows(dram, u):
-            e, n = divmod(u, UNITS)
+            e, first, blocks = units[u]
             by_partition = dram[e].rearrange("(p j) x -> p j x", j=ROWS_PER_PARTITION)
-            return by_partition[:, BLOCKS * n : BLOCKS * (n + 1), :]
+            return by_partition[:, first : first + blocks, :]
+
+        def load_w3_pass(e, g):
+            if g == 0:
+                w3_raw = weights.tile([P, 2 * PASSES1, 2 * K2], BF16)
+                raw_w3[e] = w3_raw
+            nc.sync.dma_start(
+                out=raw_w3[e][:, 2 * g : 2 * (g + 1), :],
+                in_=W3[e, K_PASS * g : K_PASS * (g + 1), :].rearrange(
+                    "(a q r) c -> q a (r c)", q=P, r=2
+                ),
+            )
 
         def load_w3(e):
-            w3_raw = weights.tile([P, 2 * PASSES1, 2 * K2], BF16)
             for g in range(PASSES1):
-                nc.sync.dma_start(
-                    out=w3_raw[:, 2 * g : 2 * (g + 1), :],
-                    in_=W3[e, K_PASS * g : K_PASS * (g + 1), :].rearrange(
-                        "(a q r) c -> q a (r c)", q=P, r=2
-                    ),
-                )
-            raw_w3[e] = w3_raw
+                load_w3_pass(e, g)
 
-        def load_w2(e):
-            w2_raw = weights.tile([P, HEADS, PACK, STATE], BF16)
-            nc.sync.dma_start(out=w2_raw[:, 0], in_=Wmu[e].rearrange("(t p) s -> p t s", p=P))
-            nc.sync.dma_start(out=w2_raw[:, 1], in_=Wsig[e].rearrange("(t p) s -> p t s", p=P))
-            raw_w2[e] = w2_raw
+        def load_w2(group):
+            w2_raw = weights.tile([P, PACK, len(group), HEADS, STATE], BF16)
+            for i, e in enumerate(group):
+                for head, dram in enumerate((Wmu, Wsig)):
+                    nc.sync.dma_start(
+                        out=w2_raw[:, :, i, head, :], in_=dram[e].rearrange("(t p) s -> p t s", p=P)
+                    )
+            raw_w2[group] = w2_raw
 
         def regroup_w3(e):
             w3_rows = raw_w3[e][:].rearrange("p a (r c) -> p (a r) c", r=2)
             w3_grouped = weights.tile([P, PASSES1, K2, PACK], BF16, align_bytes=64)
-            if e == 0:
-                for g in range(PASSES1):
-                    regroup(w3_grouped[:, g], w3_rows[:, PACK * g : PACK * (g + 1), :])
-            else:
-                nc.vector.tensor_copy(
-                    out=w3_grouped[:].rearrange("p g (c i) t -> p g c t i", i=RUN),
-                    in_=w3_rows.rearrange("p (g t) (c i) -> p g c t i", t=PACK, i=RUN),
-                )
+            nc.vector.tensor_copy(
+                out=w3_grouped[:].rearrange("p g (c i) t -> p g c t i", i=RUN),
+                in_=w3_rows.rearrange("p (g t) (c i) -> p g c t i", t=PACK, i=RUN),
+            )
             grouped_w3[e] = w3_grouped
+
+        def regroup_first_w3(g):
+            if g == 0:
+                w3_grouped = weights.tile([P, PASSES1, K2, PACK], BF16, align_bytes=64)
+                grouped_w3[0] = w3_grouped
+            w3_rows = raw_w3[0][:].rearrange("p a (r c) -> p (a r) c", r=2)
+            regroup(grouped_w3[0][:, g], w3_rows[:, PACK * g : PACK * (g + 1), :])
 
         def quantise_w3(e):
             w3_codes = weights.tile([P, PASSES1 * K2], U32, align_bytes=64)
             w3_scales = weights.tile([P, PASSES1 * K2], U8, align_bytes=64)
             if e == 0:
                 for g in range(PASSES1):
-                    cols_g = slice(g * K2, (g + 1) * K2)
+                    pass_cols = slice(g * K2, (g + 1) * K2)
                     quantise(
-                        w3_codes[:, cols_g],
-                        w3_scales[:, cols_g],
+                        w3_codes[:, pass_cols],
+                        w3_scales[:, pass_cols],
                         grouped_w3[e][:, g].rearrange("p c t -> p (c t)"),
                     )
             else:
                 quantise(w3_codes[:], w3_scales[:], grouped_w3[e][:].rearrange("p g c t -> p (g c t)"))
             stage1_weights[e] = (w3_codes, w3_scales)
 
-        def regroup_w2(e):
-            w2_grouped = weights.tile([P, HEADS, STATE, PACK], BF16, align_bytes=64)
-            nc.vector.tensor_copy(
-                out=w2_grouped[:].rearrange("p w (s i) t -> p w s t i", i=RUN),
-                in_=raw_w2[e][:].rearrange("p w t (s i) -> p w s t i", i=RUN),
-            )
-            grouped_w2[e] = w2_grouped
+        def regroup_w2(group):
+            w2_grouped = weights.tile([P, len(group) * HEADS * STATE, PACK], BF16, align_bytes=64)
+            regroup(w2_grouped[:], raw_w2[group][:].rearrange("p t e w s -> p t (e w s)"))
+            grouped_w2[group] = w2_grouped
 
-        def quantise_w2(e):
-            w2_codes = weights.tile([P, HEADS * STATE], U32, align_bytes=64)
-            w2_scales = weights.tile([P, HEADS * STATE], U8, align_bytes=64)
-            quantise(w2_codes[:], w2_scales[:], grouped_w2[e][:].rearrange("p w s t -> p (w s t)"))
-            stage2_weights[e] = (w2_codes, w2_scales)
+        def quantise_w2(group):
+            w2_codes = weights.tile([P, len(group) * HEADS * STATE], U32, align_bytes=64)
+            w2_scales = weights.tile([P, len(group) * HEADS * STATE], U8, align_bytes=64)
+            quantise(w2_codes[:], w2_scales[:], grouped_w2[group][:].rearrange("p c t -> p (c t)"))
+            stage2_weights[group] = (w2_codes, w2_scales)
+
+        def load_h2_blocks(u, first, count):
+            blocks = units[u][2]
+            if first == 0:
+                h2_raw = h2_pool.tile([P, blocks * K1], BF16)
+                h2_loaded[u] = h2_raw
+            h2_blocks = h2_loaded[u][:].rearrange("p (j k) -> p j k", j=blocks)
+            nc.sync.dma_start(
+                out=h2_blocks[:, first : first + count, :],
+                in_=batch_rows(h2, u)[:, first : first + count, :],
+            )
 
         def load_h2(u):
-            h2_raw = h2_pool.tile([P, BLOCKS * K1], BF16)
-            h2_blocks = h2_raw[:].rearrange("p (j k) -> p j k", j=BLOCKS)
-            for first in range(0, BLOCKS, PAIR):
-                nc.sync.dma_start(
-                    out=h2_blocks[:, first : first + PAIR, :],
-                    in_=batch_rows(h2, u)[:, first : first + PAIR, :],
-                )
-            h2_loaded[u] = h2_raw
+            for first in range(0, units[u][2], 2):
+                load_h2_blocks(u, first, 2)
 
         def transpose_h2(u, first_block):
+            blocks = units[u][2]
+            if first_block >= blocks:
+                return
             h2_words = h2_loaded[u][:].bitcast(F32)
             if first_block == 0:
-                h2_grouped = work.tile([P, PASSES1 * UNIT * PACK], BF16, align_bytes=64)
+                h2_grouped = work.tile([P, PASSES1 * blocks * P * PACK], BF16, align_bytes=64)
                 h2_regrouped[u] = h2_grouped
             h2_grouped_words = (
                 h2_regrouped[u][:].bitcast(F32).rearrange("p (g b u) -> p g b u", g=PASSES1, u=2)
             )
-            for j in range(first_block, first_block + PAIR):
+            for j in range(first_block, first_block + 2):
                 flipped = psum.tile([P, 2 * PASSES1, P], F32, tag="bank")
                 for a in range(2 * PASSES1):
                     first = j * WORDS + a * P
@@ -172,25 +195,32 @@ def tile_ensembledynamicmodel_pa_t_kernel(
                 )
 
         def quantise_h2(u):
-            h2_codes = work.tile([P, PASSES1 * UNIT], U32, align_bytes=64)
-            h2_scales = work.tile([P, PASSES1 * UNIT], U8, align_bytes=64)
+            columns = units[u][2] * P
+            h2_codes = work.tile([P, PASSES1 * columns], U32, align_bytes=64)
+            h2_scales = work.tile([P, PASSES1 * columns], U8, align_bytes=64)
             quantise(h2_codes[:], h2_scales[:], h2_regrouped[u][:])
             h2_quantised[u] = (h2_codes, h2_scales)
 
         def stage1(u, first_tile):
-            e = u // UNITS
+            e, first_row, blocks = units[u]
+            columns = blocks * P
             w3_codes, w3_scales = stage1_weights[e]
             h2_codes, h2_scales = h2_quantised[u]
             if first_tile == 0:
-                h_tiles = work.tile([P, H_TILES, UNIT], BF16)
+                h_tiles = work.tile([P, H_TILES, columns], BF16)
                 h_plain[u] = h_tiles
-            for m in range(first_tile, first_tile + PAIR):
-                acc1 = psum.tile([P, UNIT], F32, tag="bank")
+            accumulated = []
+            for m in range(first_tile, first_tile + 2):
+                if columns == BANK or m == first_tile:
+                    bank = psum.tile([P, BANK], F32, tag="bank")
+                    acc1 = bank[:, 0:columns]
+                else:
+                    acc1 = bank[:, columns : 2 * columns]
                 for g in range(PASSES1):
                     w_cols = slice(g * K2 + m * P, g * K2 + (m + 1) * P)
-                    x_cols = slice(g * UNIT, (g + 1) * UNIT)
+                    x_cols = slice(g * columns, (g + 1) * columns)
                     nc.tensor.matmul_mx(
-                        out=acc1[:],
+                        out=acc1,
                         lhsT=w3_codes[:, w_cols].bitcast(FP8X4),
                         lhsT_scale=w3_scales[:, w_cols],
                         rhs=h2_codes[:, x_cols].bitcast(FP8X4),
@@ -198,36 +228,46 @@ def tile_ensembledynamicmodel_pa_t_kernel(
                         start=(g == 0),
                         stop=(g == PASSES1 - 1),
                     )
+                accumulated.append((m, acc1))
+            for m, acc1 in accumulated:
                 b3_col = ROW_B3 + e * H_TILES + m
                 nc.scalar.activation(
                     out=h_plain[u][:, m, :],
-                    in_=acc1[:],
+                    in_=acc1,
                     func=ACT.Silu,
                     bias=cols[:, b3_col : b3_col + 1],
                     scale=1.0,
                 )
 
         def regroup_h(u):
-            h_grouped = work.tile([P, UNIT, PACK], BF16, align_bytes=64)
+            h_grouped = work.tile([P, units[u][2] * P, PACK], BF16, align_bytes=64)
             regroup(h_grouped[:], h_plain[u][:])
             h_regrouped[u] = h_grouped
 
         def quantise_h(u):
-            h_codes = work.tile([P, UNIT], U32, align_bytes=64)
-            h_scales = work.tile([P, UNIT], U8, align_bytes=64)
+            columns = units[u][2] * P
+            h_codes = work.tile([P, columns], U32, align_bytes=64)
+            h_scales = work.tile([P, columns], U8, align_bytes=64)
             quantise(h_codes[:], h_scales[:], h_regrouped[u][:].rearrange("p b t -> p (b t)"))
             h_quantised[u] = (h_codes, h_scales)
 
         def stage2(u):
-            e = u // UNITS
-            w2_codes, w2_scales = stage2_weights[e]
+            e, first_row, blocks = units[u]
+            columns = blocks * P
+            group = group_of[e]
+            w2_codes, w2_scales = stage2_weights[group]
             h_codes, h_scales = h_quantised[u]
             products = []
             for head in range(HEADS):
-                acc2 = psum.tile([P, UNIT], F32, tag="bank")
-                w_cols = slice(head * STATE, (head + 1) * STATE)
+                if columns == BANK or head == 0:
+                    bank = psum.tile([P, BANK], F32, tag="bank")
+                    acc2 = bank[:, 0:columns]
+                else:
+                    acc2 = bank[:, columns : 2 * columns]
+                first = (group.index(e) * HEADS + head) * STATE
+                w_cols = slice(first, first + STATE)
                 nc.tensor.matmul_mx(
-                    out=acc2[:],
+                    out=acc2,
                     lhsT=w2_codes[:, w_cols].bitcast(FP8X4),
                     lhsT_scale=w2_scales[:, w_cols],
                     rhs=h_codes[:].bitcast(FP8X4),
@@ -236,24 +276,24 @@ def tile_ensembledynamicmodel_pa_t_kernel(
                     stop=True,
                 )
                 products.append(acc2)
-            mu_t = work.tile([P, UNIT], F32)
-            nc.scalar.activation(
-                out=mu_t[:],
-                in_=products[0][:],
-                func=ACT.Identity,
-                bias=cols[:, ROW_BMU + e : ROW_BMU + e + 1],
-                scale=1.0,
-            )
-            mu_transposed[u] = mu_t
-            sigma_t = work.tile([P, UNIT], F32)
+            sigma_t = work.tile([P, columns], F32)
             nc.scalar.activation(
                 out=sigma_t[:],
-                in_=products[1][:],
+                in_=products[1],
                 func=ACT.Tanh,
                 bias=tanh_bias[:, e : e + 1],
                 scale=0.5,
             )
             sigma_transposed[u] = sigma_t
+            mu_t = work.tile([P, columns], F32)
+            nc.scalar.activation(
+                out=mu_t[:],
+                in_=products[0],
+                func=ACT.Identity,
+                bias=cols[:, ROW_BMU + e : ROW_BMU + e + 1],
+                scale=1.0,
+            )
+            mu_transposed[u] = mu_t
 
         def scale_sigma(u):
             sigma_t = sigma_transposed[u]
@@ -266,36 +306,36 @@ def tile_ensembledynamicmodel_pa_t_kernel(
                 op1=ALU.add,
             )
 
-        def flip_back(transposed):
-            back = psum.tile([P, BLOCKS, STATE], F32, tag="bank")
-            for j in range(BLOCKS):
+        def flip_back(transposed, blocks):
+            back = psum.tile([P, blocks, STATE], F32, tag="bank")
+            for j in range(blocks):
                 nc.tensor.transpose(back[:, j, :], transposed[:, j * P : (j + 1) * P], ident_f32[:])
             return back
 
         def flip_mu(u):
-            mu_banks[u] = flip_back(mu_transposed[u])
+            mu_banks[u] = flip_back(mu_transposed[u], units[u][2])
 
         def flip_sigma(u):
-            sigma_banks[u] = flip_back(sigma_transposed[u])
+            sigma_banks[u] = flip_back(sigma_transposed[u], units[u][2])
 
         def store_mu(u):
-            n = u % UNITS
-            mu_out = results.tile([P, BLOCKS, STATE], F32)
+            first, blocks = units[u][1:]
+            mu_out = results.tile([P, blocks, STATE], F32)
             nc.vector.tensor_tensor(
                 out=mu_out[:],
                 in0=mu_banks[u][:],
-                in1=state_sb[:, BLOCKS * n : BLOCKS * (n + 1), :],
+                in1=state_sb[:, first : first + blocks, :],
                 op=ALU.add,
             )
             nc.sync.dma_start(out=batch_rows(out_0, u), in_=mu_out[:])
 
         def store_sigma(u):
-            sigma_out = results.tile([P, BLOCKS, STATE], F32)
+            sigma_out = results.tile([P, units[u][2], STATE], F32)
             nc.scalar.copy(out=sigma_out[:], in_=sigma_banks[u][:])
             nc.sync.dma_start(out=batch_rows(out_1, u), in_=sigma_out[:])
 
-        load_w3(0)
-
+        load_w3_pass(0, 0)
+        load_h2_blocks(0, 0, 2)
         ident_f32 = consts.tile([P, P], F32)
         make_identity(nc, ident_f32[:])
         ident_bf16 = consts.tile([P, P], BF16)
@@ -303,7 +343,6 @@ def tile_ensembledynamicmodel_pa_t_kernel(
 
         rows = consts.tile([P, P], BF16)
         nc.vector.memset(rows[:], 0.0)
-        nc.scalar.activation(out=table_warmer[:], in_=rows[:, 0:1], func=ACT.Exp)
         nc.scalar.dma_start(
             out=rows[ROW_B3:ROW_BMU, :], in_=b3.rearrange("e (t p) -> (e t) p", p=P)
         )
@@ -315,16 +354,25 @@ def tile_ensembledynamicmodel_pa_t_kernel(
         nc.scalar.dma_start(
             out=rows[ROW_MIN : ROW_MIN + 1, :], in_=min_logstd.rearrange("(o s) -> o s", o=1)
         )
-        load_h2(0)
+        table_warmer = consts.tile([P, 1], F32)
+        nc.scalar.activation(out=table_warmer[:], in_=ident_f32[:, 0:1], func=ACT.Exp)
+        load_w3_pass(0, 1)
+        load_h2_blocks(0, 2, 2)
         load_w3(1)
         load_h2(1)
+        load_h2(2)
+        load_w2(W2_GROUPS[0])
+        load_h2(3)
         state_sb = consts.tile([P, ROWS_PER_PARTITION, STATE], BF16)
         nc.sync.dma_start(
             out=state_sb[:], in_=state.rearrange("(p j) s -> p j s", j=ROWS_PER_PARTITION)
         )
 
-        regroup_w3(0)
-        quantise_w3(0)
+        cols = consts.tile([P, P], F32)
+        tanh_bias = consts.tile([P, MEMBERS], F32)
+        exp_bounds = consts.tile([P, 2], F32)
+        sigma_scale = consts.tile([P, 1], F32)
+        sigma_shift = consts.tile([P, 1], F32)
 
         def small_vectors():
             cols_ps = psum.tile([P, P], BF16, tag="bank")
@@ -351,31 +399,57 @@ def tile_ensembledynamicmodel_pa_t_kernel(
             )
             nc.scalar.activation(out=table_warmer[:], in_=sigma_shift[:], func=ACT.Silu)
 
-        def for_unit(stage, u, *args):
-            if 0 <= u < N_UNITS:
-                stage(u, *args)
+        last = len(units) - 1
+        steps = [(u,) for u in range(last - 1)] + [(last - 1, last)]
 
-        def for_member(stage, first_unit):
-            if first_unit % UNITS == 0 and 0 <= first_unit < N_UNITS:
-                stage(first_unit // UNITS)
+        def of_step(s):
+            return steps[s] if 0 <= s < len(steps) else ()
 
-        for s in range(-2, N_UNITS + 2):
-            for_unit(load_h2, s + 4)
-            for_member(load_w2, s + 2)
-            for_member(load_w3, s + 5)
-            for_member(regroup_w3, s + 3)
-            if s + 2 > 0:
-                for_member(quantise_w3, s + 2)
-            for_member(regroup_w2, s)
-            for first in range(0, BLOCKS, PAIR):
-                for_unit(stage1, s, first)
-                for_unit(transpose_h2, s + 2, first)
-            if s == -2:
-                small_vectors()
+        def for_unit(stage, s):
+            for u in of_step(s):
+                stage(u)
+
+        def halves(items):
+            cut = (len(items) + 1) // 2
+            return items[:cut], items[cut:]
+
+        def for_member(stage, u, skip=()):
+            for e in range(MEMBERS):
+                if first_unit[e] == u and e not in skip:
+                    stage(e)
+
+        def for_group(stage, u):
+            for group in W2_GROUPS:
+                if first_unit[group[0]] == u:
+                    stage(group)
+
+        regroup_first_w3(0)
+        transpose_h2(0, 0)
+        small_vectors()
+        regroup_first_w3(1)
+        quantise_w3(0)
+        transpose_h2(0, 2)
+        quantise_h2(0)
+        for s in range(-1, len(steps) + 2):
+            if s + 4 > 3:
+                for_unit(load_h2, s + 4)
+            if s > -1:
+                for_group(load_w2, s + 2)
+            for_member(load_w3, s + 5, skip=(0, 1))
+            for_member(regroup_w3, s + 3, skip=(0,))
+            for_member(quantise_w3, s + 2, skip=(0,))
+            for_group(regroup_w2, s)
+            tiles = halves([(u, m) for u in of_step(s) for m in range(0, H_TILES, 2)])
+            blocks = halves([(u, j) for u in of_step(s + 2) for j in range(0, units[u][2], 2)])
+            for i in range(2):
+                for u, m in tiles[i]:
+                    stage1(u, m)
+                for u, j in blocks[i]:
+                    transpose_h2(u, j)
             for_unit(regroup_h, s)
             for_unit(quantise_h2, s + 2)
             for_unit(quantise_h, s)
-            for_member(quantise_w2, s)
+            for_group(quantise_w2, s)
             for_unit(stage2, s - 1)
             for_unit(scale_sigma, s - 1)
             for_unit(flip_sigma, s - 2)

from contextlib import ExitStack

import concourse.mybir as mybir
from concourse.masks import make_identity

F32 = mybir.dt.float32
BF16 = mybir.dt.bfloat16
U32 = mybir.dt.uint32
U8 = mybir.dt.uint8
FP8X4 = mybir.dt.float8_e4m3fn_x4
ACT = mybir.ActivationFunctionType
ALU = mybir.AluOpType

MEMBERS = 7
BATCH = 1024
K1 = 1024
K2 = 512
STATE = 128

P = 128
PACK = 4
K_PASS = P * PACK
PASSES1 = K1 // K_PASS
H_TILES = K2 // P
ROWS_PER_PARTITION = BATCH // P
WORDS = K1 // 2
HEADS = 2
BANKS = 8
BANK = 512
RUN = 4

BLOCKS_FIRST = (4,4)
BLOCKS_MIDDLE = (4, 4)
BLOCKS_LAST = (4,2,2)
W2_GROUPS = ((0,), (1,), (2,), (3,), (4,), (5,), (6,))

ROW_B3 = 0
ROW_BMU = ROW_B3 + MEMBERS * H_TILES
ROW_BSIG = ROW_BMU + MEMBERS
ROW_MAX = ROW_BSIG + MEMBERS
ROW_MIN = ROW_MAX + 1

FLOPS = 2 * MEMBERS * BATCH * (K1 * K2 + K2 * HEADS * STATE)


def cut_into_units():
    units = []
    for e in range(MEMBERS):
        blocks = BLOCKS_FIRST if e == 0 else BLOCKS_LAST if e == MEMBERS - 1 else BLOCKS_MIDDLE
        first = 0
        for n in blocks:
            units.append((e, first, n))
            first += n
    return units


def tile_ensembledynamicmodel_pa_t_kernel(
    tc, h2, W3, b3, Wmu, bmu, Wsig, bsig, max_logstd, min_logstd, state, out_0, out_1
):
    nc = tc.nc
    units = cut_into_units()
    first_unit = {e: [u[0] for u in units].index(e) for e in range(MEMBERS)}
    group_of = {e: group for group in W2_GROUPS for e in group}

    def regroup(dst, src):
        nc.vector.tensor_copy(
            out=dst.rearrange("p (c i) t -> p c t i", i=RUN),
            in_=src.rearrange("p t (c i) -> p c t i", i=RUN),
        )

    def quantise(codes, scales, grouped):
        nc.vector.quantize_mx(out=codes.bitcast(FP8X4), scales=scales, in_=grouped)

    with ExitStack() as ctx:
        consts = ctx.enter_context(tc.tile_pool(name="consts", bufs=1))
        h2_pool = ctx.enter_context(tc.tile_pool(name="h2_pool", bufs=5))
        weights = ctx.enter_context(tc.tile_pool(name="weights", bufs=3))
        work = ctx.enter_context(tc.tile_pool(name="work", bufs=3))
        results = ctx.enter_context(tc.tile_pool(name="results", bufs=6))
        psum = ctx.enter_context(tc.psum_pool(name="psum", bufs=BANKS))
        ctx.enter_context(tc.manual_schedule())

        raw_w3, raw_w2, grouped_w3, grouped_w2, stage1_weights, stage2_weights = {}, {}, {}, {}, {}, {}
        h2_loaded, h2_regrouped, h2_quantised = {}, {}, {}
        h_plain, h_regrouped, h_quantised = {}, {}, {}
        mu_transposed, sigma_transposed, mu_banks, sigma_banks = {}, {}, {}, {}

        def batch_rows(dram, u):
            e, first, blocks = units[u]
            by_partition = dram[e].rearrange("(p j) x -> p j x", j=ROWS_PER_PARTITION)
            return by_partition[:, first : first + blocks, :]

        def load_w3_pass(e, g):
            if g == 0:
                w3_raw = weights.tile([P, 2 * PASSES1, 2 * K2], BF16)
                raw_w3[e] = w3_raw
            nc.sync.dma_start(
                out=raw_w3[e][:, 2 * g : 2 * (g + 1), :],
                in_=W3[e, K_PASS * g : K_PASS * (g + 1), :].rearrange(
                    "(a q r) c -> q a (r c)", q=P, r=2
                ),
            )

        def load_w3(e):
            for g in range(PASSES1):
                load_w3_pass(e, g)

        def load_w2(group):
            w2_raw = weights.tile([P, PACK, len(group), HEADS, STATE], BF16)
            for i, e in enumerate(group):
                for head, dram in enumerate((Wmu, Wsig)):
                    nc.sync.dma_start(
                        out=w2_raw[:, :, i, head, :], in_=dram[e].rearrange("(t p) s -> p t s", p=P)
                    )
            raw_w2[group] = w2_raw

        def regroup_w3(e):
            w3_rows = raw_w3[e][:].rearrange("p a (r c) -> p (a r) c", r=2)
            w3_grouped = weights.tile([P, PASSES1, K2, PACK], BF16, align_bytes=64)
            nc.vector.tensor_copy(
                out=w3_grouped[:].rearrange("p g (c i) t -> p g c t i", i=RUN),
                in_=w3_rows.rearrange("p (g t) (c i) -> p g c t i", t=PACK, i=RUN),
            )
            grouped_w3[e] = w3_grouped

        def regroup_first_w3(g):
            if g == 0:
                w3_grouped = weights.tile([P, PASSES1, K2, PACK], BF16, align_bytes=64)
                grouped_w3[0] = w3_grouped
            w3_rows = raw_w3[0][:].rearrange("p a (r c) -> p (a r) c", r=2)
            regroup(grouped_w3[0][:, g], w3_rows[:, PACK * g : PACK * (g + 1), :])

        def quantise_w3(e):
            w3_codes = weights.tile([P, PASSES1 * K2], U32, align_bytes=64)
            w3_scales = weights.tile([P, PASSES1 * K2], U8, align_bytes=64)
            if e == 0:
                for g in range(PASSES1):
                    pass_cols = slice(g * K2, (g + 1) * K2)
                    quantise(
                        w3_codes[:, pass_cols],
                        w3_scales[:, pass_cols],
                        grouped_w3[e][:, g].rearrange("p c t -> p (c t)"),
                    )
            else:
                quantise(w3_codes[:], w3_scales[:], grouped_w3[e][:].rearrange("p g c t -> p (g c t)"))
            stage1_weights[e] = (w3_codes, w3_scales)

        def regroup_w2(group):
            w2_grouped = weights.tile([P, len(group) * HEADS * STATE, PACK], BF16, align_bytes=64)
            regroup(w2_grouped[:], raw_w2[group][:].rearrange("p t e w s -> p t (e w s)"))
            grouped_w2[group] = w2_grouped

        def quantise_w2(group):
            w2_codes = weights.tile([P, len(group) * HEADS * STATE], U32, align_bytes=64)
            w2_scales = weights.tile([P, len(group) * HEADS * STATE], U8, align_bytes=64)
            quantise(w2_codes[:], w2_scales[:], grouped_w2[group][:].rearrange("p c t -> p (c t)"))
            stage2_weights[group] = (w2_codes, w2_scales)

        def load_h2_blocks(u, first, count):
            blocks = units[u][2]
            if first == 0:
                h2_raw = h2_pool.tile([P, blocks * K1], BF16)
                h2_loaded[u] = h2_raw
            h2_blocks = h2_loaded[u][:].rearrange("p (j k) -> p j k", j=blocks)
            nc.sync.dma_start(
                out=h2_blocks[:, first : first + count, :],
                in_=batch_rows(h2, u)[:, first : first + count, :],
            )

        def load_h2(u):
            for first in range(0, units[u][2], 2):
                load_h2_blocks(u, first, 2)

        def transpose_h2(u, first_block):
            blocks = units[u][2]
            if first_block >= blocks:
                return
            h2_words = h2_loaded[u][:].bitcast(F32)
            if first_block == 0:
                h2_grouped = work.tile([P, PASSES1 * blocks * P * PACK], BF16, align_bytes=64)
                h2_regrouped[u] = h2_grouped
            h2_grouped_words = (
                h2_regrouped[u][:].bitcast(F32).rearrange("p (g b u) -> p g b u", g=PASSES1, u=2)
            )
            for j in range(first_block, first_block + 2):
                flipped = psum.tile([P, 2 * PASSES1, P], F32, tag="bank")
                for a in range(2 * PASSES1):
                    first = j * WORDS + a * P
                    nc.tensor.transpose(
                        flipped[:, a, :], h2_words[:, first : first + P], ident_f32[:]
                    )
                nc.scalar.copy(
                    out=h2_grouped_words[:, :, j * P : (j + 1) * P, :],
                    in_=flipped[:].rearrange("p (g u) b -> p g b u", u=2),
                )

        def quantise_h2(u):
            columns = units[u][2] * P
            h2_codes = work.tile([P, PASSES1 * columns], U32, align_bytes=64)
            h2_scales = work.tile([P, PASSES1 * columns], U8, align_bytes=64)
            quantise(h2_codes[:], h2_scales[:], h2_regrouped[u][:])
            h2_quantised[u] = (h2_codes, h2_scales)

        def stage1(u, first_tile):
            e, first_row, blocks = units[u]
            columns = blocks * P
            w3_codes, w3_scales = stage1_weights[e]
            h2_codes, h2_scales = h2_quantised[u]
            if first_tile == 0:
                h_tiles = work.tile([P, H_TILES, columns], BF16)
                h_plain[u] = h_tiles
            accumulated = []
            for m in range(first_tile, first_tile + 2):
                if columns == BANK or m == first_tile:
                    bank = psum.tile([P, BANK], F32, tag="bank")
                    acc1 = bank[:, 0:columns]
                else:
                    acc1 = bank[:, columns : 2 * columns]
                for g in range(PASSES1):
                    w_cols = slice(g * K2 + m * P, g * K2 + (m + 1) * P)
                    x_cols = slice(g * columns, (g + 1) * columns)
                    nc.tensor.matmul_mx(
                        out=acc1,
                        lhsT=w3_codes[:, w_cols].bitcast(FP8X4),
                        lhsT_scale=w3_scales[:, w_cols],
                        rhs=h2_codes[:, x_cols].bitcast(FP8X4),
                        rhs_scale=h2_scales[:, x_cols],
                        start=(g == 0),
                        stop=(g == PASSES1 - 1),
                    )
                accumulated.append((m, acc1))
            for m, acc1 in accumulated:
                b3_col = ROW_B3 + e * H_TILES + m
                nc.scalar.activation(
                    out=h_plain[u][:, m, :],
                    in_=acc1,
                    func=ACT.Silu,
                    bias=cols[:, b3_col : b3_col + 1],
                    scale=1.0,
                )

        def regroup_h(u):
            h_grouped = work.tile([P, units[u][2] * P, PACK], BF16, align_bytes=64)
            regroup(h_grouped[:], h_plain[u][:])
            h_regrouped[u] = h_grouped

        def quantise_h(u):
            columns = units[u][2] * P
            h_codes = work.tile([P, columns], U32, align_bytes=64)
            h_scales = work.tile([P, columns], U8, align_bytes=64)
            quantise(h_codes[:], h_scales[:], h_regrouped[u][:].rearrange("p b t -> p (b t)"))
            h_quantised[u] = (h_codes, h_scales)

        def stage2(u):
            e, first_row, blocks = units[u]
            columns = blocks * P
            group = group_of[e]
            w2_codes, w2_scales = stage2_weights[group]
            h_codes, h_scales = h_quantised[u]
            products = []
            for head in range(HEADS):
                if columns == BANK or head == 0:
                    bank = psum.tile([P, BANK], F32, tag="bank")
                    acc2 = bank[:, 0:columns]
                else:
                    acc2 = bank[:, columns : 2 * columns]
                first = (group.index(e) * HEADS + head) * STATE
                w_cols = slice(first, first + STATE)
                nc.tensor.matmul_mx(
                    out=acc2,
                    lhsT=w2_codes[:, w_cols].bitcast(FP8X4),
                    lhsT_scale=w2_scales[:, w_cols],
                    rhs=h_codes[:].bitcast(FP8X4),
                    rhs_scale=h_scales[:],
                    start=True,
                    stop=True,
                )
                products.append(acc2)
            sigma_t = work.tile([P, columns], F32)
            nc.scalar.activation(
                out=sigma_t[:],
                in_=products[1],
                func=ACT.Tanh,
                bias=tanh_bias[:, e : e + 1],
                scale=0.5,
            )
            sigma_transposed[u] = sigma_t
            mu_t = work.tile([P, columns], F32)
            nc.scalar.activation(
                out=mu_t[:],
                in_=products[0],
                func=ACT.Identity,
                bias=cols[:, ROW_BMU + e : ROW_BMU + e + 1],
                scale=1.0,
            )
            mu_transposed[u] = mu_t

        def scale_sigma(u):
            sigma_t = sigma_transposed[u]
            nc.vector.tensor_scalar(
                out=sigma_t[:],
                in0=sigma_t[:],
                scalar1=sigma_scale[:, 0:1],
                scalar2=sigma_shift[:, 0:1],
                op0=ALU.mult,
                op1=ALU.add,
            )

        def flip_back(transposed, blocks):
            back = psum.tile([P, blocks, STATE], F32, tag="bank")
            for j in range(blocks):
                nc.tensor.transpose(back[:, j, :], transposed[:, j * P : (j + 1) * P], ident_f32[:])
            return back

        def flip_mu(u):
            mu_banks[u] = flip_back(mu_transposed[u], units[u][2])

        def flip_sigma(u):
            sigma_banks[u] = flip_back(sigma_transposed[u], units[u][2])

        def store_mu(u):
            first, blocks = units[u][1:]
            mu_out = results.tile([P, blocks, STATE], F32)
            nc.vector.tensor_tensor(
                out=mu_out[:],
                in0=mu_banks[u][:],
                in1=state_sb[:, first : first + blocks, :],
                op=ALU.add,
            )
            nc.sync.dma_start(out=batch_rows(out_0, u), in_=mu_out[:])

        def store_sigma(u):
            sigma_out = results.tile([P, units[u][2], STATE], F32)
            nc.scalar.copy(out=sigma_out[:], in_=sigma_banks[u][:])
            nc.sync.dma_start(out=batch_rows(out_1, u), in_=sigma_out[:])

        load_w3_pass(0, 0)
        load_h2_blocks(0, 0, 2)
        ident_f32 = consts.tile([P, P], F32)
        make_identity(nc, ident_f32[:])
        ident_bf16 = consts.tile([P, P], BF16)
        make_identity(nc, ident_bf16[:])

        rows = consts.tile([P, P], BF16)
        nc.vector.memset(rows[:], 0.0)
        nc.scalar.dma_start(
            out=rows[ROW_B3:ROW_BMU, :], in_=b3.rearrange("e (t p) -> (e t) p", p=P)
        )
        nc.scalar.dma_start(out=rows[ROW_BMU:ROW_BSIG, :], in_=bmu)
        nc.scalar.dma_start(out=rows[ROW_BSIG:ROW_MAX, :], in_=bsig)
        nc.scalar.dma_start(
            out=rows[ROW_MAX : ROW_MAX + 1, :], in_=max_logstd.rearrange("(o s) -> o s", o=1)
        )
        nc.scalar.dma_start(
            out=rows[ROW_MIN : ROW_MIN + 1, :], in_=min_logstd.rearrange("(o s) -> o s", o=1)
        )
        table_warmer = consts.tile([P, 1], F32)
        nc.scalar.activation(out=table_warmer[:], in_=ident_f32[:, 0:1], func=ACT.Exp)
        load_w3_pass(0, 1)
        load_h2_blocks(0, 2, 2)
        load_w3(1)
        load_h2(1)
        load_h2(2)
        load_w2(W2_GROUPS[0])
        load_h2(3)
        state_sb = consts.tile([P, ROWS_PER_PARTITION, STATE], BF16)
        nc.sync.dma_start(
            out=state_sb[:], in_=state.rearrange("(p j) s -> p j s", j=ROWS_PER_PARTITION)
        )

        cols = consts.tile([P, P], F32)
        tanh_bias = consts.tile([P, MEMBERS], F32)
        exp_bounds = consts.tile([P, 2], F32)
        sigma_scale = consts.tile([P, 1], F32)
        sigma_shift = consts.tile([P, 1], F32)

        def small_vectors():
            cols_ps = psum.tile([P, P], BF16, tag="bank")
            nc.tensor.transpose(cols_ps[:], rows[:], ident_bf16[:])
            nc.vector.tensor_copy(out=cols[:], in_=cols_ps[:])
            nc.vector.tensor_scalar(
                out=tanh_bias[:],
                in0=cols[:, ROW_BSIG:ROW_MAX],
                scalar1=cols[:, ROW_MAX : ROW_MAX + 1],
                scalar2=0.5,
                op0=ALU.subtract,
                op1=ALU.mult,
            )
            nc.scalar.activation(
                out=exp_bounds[:], in_=cols[:, ROW_MAX : ROW_MIN + 1], func=ACT.Exp
            )
            nc.scalar.mul(out=sigma_scale[:], in_=exp_bounds[:, 0:1], mul=0.5)
            nc.scalar.activation(
                out=sigma_shift[:],
                in_=exp_bounds[:, 1:2],
                func=ACT.Identity,
                bias=sigma_scale[:, 0:1],
                scale=1.0,
            )
            nc.scalar.activation(out=table_warmer[:], in_=sigma_shift[:], func=ACT.Silu)

        last = len(units) - 1
        steps = [(u,) for u in range(last - 1)] + [(last - 1, last)]

        def of_step(s):
            return steps[s] if 0 <= s < len(steps) else ()

        def for_unit(stage, s):
            for u in of_step(s):
                stage(u)

        def halves(items):
            cut = (len(items) + 1) // 2
            return items[:cut], items[cut:]

        def for_member(stage, u, skip=()):
            for e in range(MEMBERS):
                if first_unit[e] == u and e not in skip:
                    stage(e)

        def for_group(stage, u):
            for group in W2_GROUPS:
                if first_unit[group[0]] == u:
                    stage(group)

        regroup_first_w3(0)
        transpose_h2(0, 0)
        small_vectors()
        regroup_first_w3(1)
        quantise_w3(0)
        transpose_h2(0, 2)
        quantise_h2(0)
        for s in range(-1, len(steps) + 2):
            if s + 4 > 3:
                for_unit(load_h2, s + 4)
            if s > -1:
                for_group(load_w2, s + 2)
            for_member(load_w3, s + 5, skip=(0, 1))
            for_member(regroup_w3, s + 3, skip=(0,))
            for_member(quantise_w3, s + 2, skip=(0,))
            for_group(regroup_w2, s)
            tiles = halves([(u, m) for u in of_step(s) for m in range(0, H_TILES, 2)])
            blocks = halves([(u, j) for u in of_step(s + 2) for j in range(0, units[u][2], 2)])
            for i in range(2):
                for u, m in tiles[i]:
                    stage1(u, m)
                for u, j in blocks[i]:
                    transpose_h2(u, j)
            for_unit(regroup_h, s)
            for_unit(quantise_h2, s + 2)
            for_unit(quantise_h, s)
            for_group(quantise_w2, s)
            for_unit(stage2, s - 1)
            for_unit(scale_sigma, s - 1)
            for_unit(flip_sigma, s - 2)
            for_unit(flip_mu, s - 2)
            for_unit(store_sigma, s - 2)
            for_unit(store_mu, s - 2)
